import numpy as np
import ml_dtypes


def mxq(x, axis, fmt="e4m3"):
    dtype, down = {"e4m3": (ml_dtypes.float8_e4m3fn, 7), "e5m2": (ml_dtypes.float8_e5m2, 14)}[fmt]
    v = np.moveaxis(np.asarray(x, np.float32).astype(ml_dtypes.bfloat16).astype(np.float64), axis, -1)
    blocks = v.reshape(v.shape[:-1] + (-1, 32))
    amax = np.abs(blocks).max(-1, keepdims=True)
    byte = np.maximum(np.where(amax > 0, np.frexp(amax)[1] - 1 + 127, 0) - down, 1)
    scale = np.exp2(byte - 127.0)
    codes = (blocks / scale).astype(np.float32).astype(dtype).astype(np.float64)
    return np.moveaxis((codes * scale).reshape(v.shape), -1, axis)


WIDE = False


def mx_kscale(k):
    if not WIDE:
        return np.ones(k)
    levels = np.array([10, -10, 5, -5, 0])
    if k % 512:
        return np.exp2(np.random.permutation(np.resize(levels, k // 32))).repeat(32)
    a = np.empty((k // 512, 16))
    for p in range(k // 512):
        a[p, :8] = np.random.permutation(np.resize(levels, 8))
        for g in range(8):
            far = levels[np.abs(levels - a[p, g]) >= 10]
            a[p, g + 8] = far[np.random.randint(len(far))]
    return np.exp2(a.ravel()).repeat(32)


BF16 = ml_dtypes.bfloat16


def bf(x):
    return np.asarray(x, np.float32).astype(BF16)


def f64(x):
    return np.asarray(x).astype(np.float64)


B, P, D, NL, T, E, G = 8, 512, 512, 8, 2, 1, 2
WG = NL * NL * T * G
CLIP = 1.0
LOG_2PI = np.log(2.0 * np.pi)


def clip(v):
    return np.clip(v, -CLIP, CLIP)


def gaussian_multi(m1, v1, m2, v2):
    v1s = np.exp(2.0 * v1)
    v2s = np.exp(2.0 * v2)
    add = v1s + v2s
    log_add = np.log(add)
    scale = (-0.5 * (LOG_2PI + log_add + (m1 - m2) ** 2 / add)).sum(-1)
    mu = (m1 * v2s + m2 * v1s) / add
    var = v1 + v2 - 0.5 * log_add
    return scale, mu, var


def setup_inputs():
    s = mx_kscale(D)
    return {"x": bf(np.random.standard_normal((B, P, D)) * s),
            "s_weight": bf(np.random.standard_normal((B, P, NL, E))),
            "s_mu": bf(clip(np.random.standard_normal((B, P, NL, E, G)))),
            "s_var": bf(clip(np.random.standard_normal((B, P, NL, E, G)))),
            "tcm_w": bf(np.random.standard_normal((D, WG)) / np.sqrt(D) / s[:, None]),
            "tcm_b": bf(np.random.standard_normal(WG) * 0.3),
            "tcv_w": bf(np.random.standard_normal((D, WG)) / np.sqrt(D) / s[:, None]),
            "tcv_b": bf(np.random.standard_normal(WG) * 0.3)}


def reference(x, s_weight, s_mu, s_var, tcm_w, tcm_b, tcv_w, tcv_b):
    xq = mxq(f64(x).reshape(B * P, D), 1, "e4m3")
    t_c_mu = clip(((xq @ mxq(f64(tcm_w), 0, "e4m3")) + f64(tcm_b)).reshape(B, P, NL, NL, T, G))[:, :, :, :, :, None, :]
    t_c_var = clip(((xq @ mxq(f64(tcv_w), 0, "e4m3")) + f64(tcv_b)).reshape(B, P, NL, NL, T, G))[:, :, :, :, :, None, :]
    m1 = f64(s_mu)[:, :, None, :, None, :, :]
    v1 = f64(s_var)[:, :, None, :, None, :, :]
    cs_scale, cs_mu, cs_var = gaussian_multi(m1, v1, t_c_mu, t_c_var)
    cs_scale = cs_scale + f64(s_weight)[:, :, None, :, None, :]
    return cs_scale, cs_mu, cs_var

@@ -1,0 +1,393 @@
+import math
+from contextlib import ExitStack
+
+import concourse.masks as masks
+import concourse.mybir as mybir
+
+F32 = mybir.dt.float32
+BF16 = mybir.dt.bfloat16
+U32 = mybir.dt.uint32
+U8 = mybir.dt.uint8
+FP8X4 = mybir.dt.float8_e4m3fn_x4
+ALU = mybir.AluOpType
+ACT = mybir.ActivationFunctionType
+
+FLOPS = 2 * 4096 * 512 * 512
+
+P = 128
+TILES = 32
+UNIT = 4
+UNITS = TILES // UNIT
+ROWS = UNIT * P
+K = 512
+NC = 256
+NI = 8
+JTG = NC // NI
+JT = JTG // 2
+BLOCKS = 2 * NC // P
+AHEAD_PROJECT = 1
+AHEAD_QUANTISE = 2
+AHEAD_TRANSPOSE = 3
+AHEAD_FRONT = 2
+AHEAD_LN = 2
+
+
+def tile_chainlveg_pa_t_kernel(
+    tc, x, s_weight, s_mu, s_var, tcm_w, tcm_b, tcv_w, tcv_b, out_0, out_1, out_2
+):
+    nc = tc.nc
+    x_rows = x.rearrange("b (c n) k -> (b c) n k", n=TILES)
+    scale_rows = out_0.rearrange("b (c n) i j t e -> (b c) n (i j t e)", n=TILES)
+    mu_rows = out_1.rearrange("b (c n) i j t e g -> (b c) n (i j t e g)", n=TILES)
+    var_rows = out_2.rearrange("b (c n) i j t e g -> (b c) n (i j t e g)", n=TILES)
+
+    with ExitStack() as ctx:
+        keep = ctx.enter_context(tc.tile_pool(name="keep", bufs=1))
+        grouped_pool = ctx.enter_context(tc.tile_pool(name="grouped", bufs=2))
+        xq_pool = ctx.enter_context(tc.tile_pool(name="xq", bufs=3))
+        ym_pool = ctx.enter_context(tc.tile_pool(name="ym", bufs=2))
+        yv_pool = ctx.enter_context(tc.tile_pool(name="yv", bufs=UNITS))
+        da_pool = ctx.enter_context(tc.tile_pool(name="da", bufs=3))
+        out_pool = ctx.enter_context(tc.tile_pool(name="outs", bufs=3))
+        sum_pool = ctx.enter_context(tc.tile_pool(name="sums", bufs=2))
+        psum = ctx.enter_context(tc.psum_pool(name="psum", bufs=4))
+        ctx.enter_context(tc.manual_schedule())
+
+        def tiles_of(s):
+            return slice(s * UNIT, (s + 1) * UNIT)
+
+        x_sb = keep.tile([P, TILES, K], BF16, name="x_sb")
+        w_raw = keep.tile([P, 4, 2 * NC], BF16, name="w_raw")
+        bias_rows = keep.tile([P, P], BF16, name="bias_rows")
+        smu = keep.tile([P, TILES * 16], BF16, name="smu")
+        svar = keep.tile([P, TILES * 16], BF16, name="svar")
+        sw = keep.tile([P, TILES * 8], BF16, name="sw")
+        nc.vector.memset(bias_rows[:], 0.0)
+        for w, first_column in ((tcm_w, 0), (tcv_w, NC)):
+            nc.sync.dma_start(
+                out=w_raw[:, :, first_column : first_column + NC],
+                in_=w.rearrange("(q t) c -> q t c", t=4),
+            )
+        nc.scalar.dma_start(
+            out=svar[:], in_=s_var.rearrange("b (c n) j e g -> (b c) (n j e g)", n=TILES)
+        )
+        nc.scalar.dma_start(out=x_sb[:, 0 : UNIT // 2, :], in_=x_rows[:, 0 : UNIT // 2, :])
+        nc.scalar.dma_start(out=x_sb[:, UNIT // 2 : UNIT, :], in_=x_rows[:, UNIT // 2 : UNIT, :])
+        nc.scalar.dma_start(out=bias_rows[0:2, :], in_=tcm_b.rearrange("(r c) -> r c", r=2))
+        nc.scalar.dma_start(out=bias_rows[2:4, :], in_=tcv_b.rearrange("(r c) -> r c", r=2))
+        nc.scalar.dma_start(
+            out=smu[:], in_=s_mu.rearrange("b (c n) j e g -> (b c) (n j e g)", n=TILES)
+        )
+        nc.sync.dma_start(out=x_sb[:, tiles_of(1), :], in_=x_rows[:, tiles_of(1), :])
+        nc.scalar.dma_start(
+            out=sw[:], in_=s_weight.rearrange("b (c n) j e -> (b c) (n j e)", n=TILES)
+        )
+        for s in range(2, UNITS):
+            nc.sync.dma_start(out=x_sb[:, tiles_of(s), :], in_=x_rows[:, tiles_of(s), :])
+
+        ident = keep.tile([P, P], F32, name="ident")
+        masks.make_identity(nc, ident[:])
+        minus_one = keep.tile([P, 1], F32, name="minus_one")
+        nc.vector.memset(minus_one[:], -1.0)
+        w_grouped = keep.tile([P, 2 * NC, 4], BF16, name="w_grouped", align_bytes=64)
+        w_codes = keep.tile([P, 2 * NC], U32, name="w_codes", align_bytes=64)
+        w_scales = keep.tile([P, 2 * NC], U8, name="w_scales", align_bytes=64)
+        bias_f32 = keep.tile([P, P], F32, name="bias_f32")
+        bias_plus_1 = keep.tile([P, BLOCKS], F32, name="bias_plus_1")
+        work = keep.tile([P, TILES, 2 * NC], F32, name="work")
+        m1 = keep.tile([P, TILES, JTG], F32, name="m1")
+        m1_plus_1 = keep.tile([P, TILES, JTG], F32, name="m1_plus_1")
+        v1_plus_1 = keep.tile([P, TILES, JTG], F32, name="v1_plus_1")
+        half_inv_a = keep.tile([P, TILES, JTG], F32, name="half_inv_a")
+        v1_sum = keep.tile([P, TILES * 8], F32, name="v1_sum")
+        offset_j = keep.tile([P, TILES * 8], F32, name="offset_j")
+        offset = keep.tile([P, TILES, JT], F32, name="offset")
+
+        alive = {}
+
+        def repeat_t(small):
+            return (
+                small[:]
+                .rearrange("p (a g) -> p a g", g=2)
+                .unsqueeze(2)
+                .to_broadcast([P, TILES * 8, 2, 2])
+            )
+
+        def as_njtg(full):
+            return full[:].rearrange("p n (j t g) -> p (n j) t g", t=2, g=2)
+
+        def by_i(ap):
+            return ap.rearrange("p (i c) -> p i c", i=NI)
+
+        def by_tile_and_i(ap):
+            return ap.rearrange("p n (i c) -> p n i c", i=NI)
+
+        def repeat_i(small, n, count):
+            width = small.shape[2]
+            return small[:, n : n + count, :].unsqueeze(2).to_broadcast([P, count, NI, width])
+
+        def halves(s):
+            return [(lo, s * UNIT + lo, UNIT // 2) for lo in range(0, UNIT, UNIT // 2)]
+
+        def quantise_weights():
+            for first_column in (0, NC):
+                columns = slice(first_column, first_column + NC)
+                nc.vector.tensor_copy(
+                    out=w_grouped[:, columns, :],
+                    in_=w_raw[:, :, columns].rearrange("p t c -> p c t"),
+                )
+            for first_column in (0, NC):
+                columns = slice(first_column, first_column + NC)
+                nc.vector.quantize_mx(
+                    out=w_codes[:, columns].bitcast(FP8X4),
+                    scales=w_scales[:, columns],
+                    in_=w_grouped[:, columns, :].rearrange("p c t -> p (c t)"),
+                )
+
+        def bias_to_partitions():
+            nc.vector.tensor_copy(out=bias_f32[:], in_=bias_rows[:])
+            turned = psum.tile([P, 512], F32, name="turned", tag="to_scalar")
+            nc.tensor.transpose(turned[:, 0:P], bias_f32[:], ident[:])
+            nc.vector.tensor_scalar_add(
+                out=bias_plus_1[:], in0=turned[:, 0:BLOCKS], scalar1=1.0
+            )
+
+        def spread_state():
+            nc.vector.tensor_scalar_add(out=as_njtg(v1_plus_1), in0=repeat_t(svar), scalar1=1.0)
+            nc.vector.tensor_copy(out=as_njtg(m1), in_=repeat_t(smu))
+            nc.vector.tensor_scalar_add(out=m1_plus_1[:], in0=m1[:], scalar1=1.0)
+            nc.vector.tensor_scalar_mul(out=half_inv_a[:], in0=half_inv_a[:], scalar1=0.5)
+
+        def scale_offset():
+            pairs = svar[:].rearrange("p (a g) -> p a g", g=2)
+            nc.vector.tensor_tensor(
+                out=v1_sum[:], in0=pairs[:, :, 0], in1=pairs[:, :, 1], op=ALU.add
+            )
+            nc.vector.scalar_tensor_tensor(
+                out=offset_j[:], in0=sw[:], scalar=2.0 - math.log(2.0 * math.pi), in1=v1_sum[:],
+                op0=ALU.add, op1=ALU.subtract,
+            )
+            nc.vector.tensor_copy(
+                out=offset[:].rearrange("p n (j t) -> p (n j) t", t=2),
+                in_=offset_j[:].unsqueeze(2).to_broadcast([P, TILES * 8, 2]),
+            )
+
+        def transpose_x(s):
+            grouped = grouped_pool.tile([P, 4 * ROWS], BF16, name="grouped", align_bytes=64)
+            alive[("grouped", s)] = grouped
+            for lo in range(0, UNIT, 2):
+                turned = psum.tile([P, 2, 2 * P], F32, name="x_turned", tag="to_scalar")
+                for j in range(2):
+                    words = x_sb[:, s * UNIT + lo + j, :].bitcast(F32)
+                    for u in range(2):
+                        nc.tensor.transpose(
+                            turned[:, u, j * P : (j + 1) * P],
+                            words[:, u : 2 * P : 2],
+                            ident[:],
+                        )
+                nc.scalar.copy(
+                    out=grouped[:].bitcast(F32)[:, lo * 2 * P : (lo + 2) * 2 * P].rearrange(
+                        "p (r u) -> p r u", u=2
+                    ),
+                    in_=turned[:].rearrange("p u r -> p r u"),
+                )
+
+        def quantise_x(s):
+            codes = xq_pool.tile([P, ROWS], U32, name="x_codes", align_bytes=64)
+            scales = xq_pool.tile([P, ROWS], U8, name="x_scales", align_bytes=64)
+            alive[("xq", s)] = (codes, scales)
+            nc.vector.quantize_mx(
+                out=codes[:].bitcast(FP8X4), scales=scales[:], in_=alive[("grouped", s)][:]
+            )
+
+        def project(s):
+            codes, scales = alive[("xq", s)]
+            y = (
+                ym_pool.tile([P, 2, ROWS], F32, name="ym"),
+                yv_pool.tile([P, 2, ROWS], F32, name="yv"),
+            )
+            alive[("y", s)] = y
+            for block in range(BLOCKS):
+                columns = slice(block * P, (block + 1) * P)
+                product = psum.tile([P, ROWS], F32, name="product", tag="to_scalar")
+                nc.tensor.matmul_mx(
+                    out=product[:],
+                    lhsT=w_codes[:, columns].bitcast(FP8X4),
+                    lhsT_scale=w_scales[:, columns],
+                    rhs=codes[:].bitcast(FP8X4),
+                    rhs_scale=scales[:],
+                    start=True,
+                    stop=True,
+                )
+                nc.scalar.activation(
+                    out=y[block // 2][:, block % 2, :], in_=product[:], func=ACT.Relu,
+                    bias=bias_plus_1[:, block : block + 1], scale=1.0,
+                )
+
+        def back_to_rows(s):
+            y = alive[("y", s)]
+            da = da_pool.tile([P, UNIT, NC], F32, name="da")
+            alive[("da", s)] = da
+            banks = []
+
+            def clip_and_subtract(lo, half, state_plus_1):
+                n = s * UNIT + lo
+                columns = slice(half * NC, (half + 1) * NC)
+                nc.vector.scalar_tensor_tensor(
+                    out=by_i(work[:, n, columns]),
+                    in0=by_i(banks[lo][:, columns]),
+                    scalar=2.0,
+                    in1=state_plus_1[:, n, :].unsqueeze(1).to_broadcast([P, NI, JTG]),
+                    op0=ALU.min,
+                    op1=ALU.subtract,
+                )
+
+            for lo in range(UNIT):
+                n = s * UNIT + lo
+                bank = psum.tile([P, 2 * NC], F32, name="y_rows", tag="to_vector")
+                banks.append(bank)
+                for block in range(BLOCKS):
+                    nc.tensor.transpose(
+                        bank[:, block * P : (block + 1) * P],
+                        y[block // 2][:, block % 2, lo * P : (lo + 1) * P],
+                        ident[:],
+                    )
+                clip_and_subtract(lo, 0, m1_plus_1)
+                nc.gpsimd.tensor_tensor(
+                    out=by_i(da[:, lo, :]),
+                    in0=by_i(work[:, n, 0:NC]),
+                    in1=half_inv_a[:, n, :].unsqueeze(1).to_broadcast([P, NI, JTG]),
+                    op=ALU.mult,
+                )
+            for lo in range(UNIT):
+                clip_and_subtract(lo, 1, v1_plus_1)
+
+        def sigmoid(s):
+            u = work[:, tiles_of(s), NC : 2 * NC]
+            nc.scalar.activation(out=u, in_=u, func=ACT.Sigmoid, scale=-2.0)
+
+        def front(s):
+            if 0 <= s < UNITS:
+                back_to_rows(s)
+            if 0 <= s + AHEAD_QUANTISE < UNITS:
+                quantise_x(s + AHEAD_QUANTISE)
+            if s == 0:
+                scale_offset()
+            if 0 <= s + AHEAD_PROJECT < UNITS:
+                project(s + AHEAD_PROJECT)
+            if 0 <= s + AHEAD_TRANSPOSE < UNITS:
+                transpose_x(s + AHEAD_TRANSPOSE)
+                if s + AHEAD_TRANSPOSE == 0:
+                    bias_to_partitions()
+            if 0 <= s < UNITS:
+                sigmoid(s)
+
+        def products(s):
+            g = out_pool.tile([P, UNIT, NC], F32, name="g")
+            da = alive[("da", s)]
+            for lo, n, count in halves(s):
+                nc.vector.tensor_tensor(
+                    out=g[:, lo : lo + count, :], in0=work[:, n : n + count, 0:NC],
+                    in1=work[:, n : n + count, NC : 2 * NC], op=ALU.mult,
+                )
+            for lo, n, count in halves(s):
+                nc.vector.tensor_tensor(
+                    out=work[:, n : n + count, 0:NC], in0=g[:, lo : lo + count, :],
+                    in1=da[:, lo : lo + count, :], op=ALU.mult,
+                )
+            for lo, n, count in halves(s):
+                nc.vector.tensor_tensor(
+                    out=by_tile_and_i(g[:, lo : lo + count, :]),
+                    in0=by_tile_and_i(g[:, lo : lo + count, :]),
+                    in1=repeat_i(m1, n, count), op=ALU.add,
+                )
+            nc.sync.dma_start(out=mu_rows[:, tiles_of(s), :], in_=g[:])
+
+        def log_weight(s):
+            wc = work[:, tiles_of(s), NC : 2 * NC]
+            nc.scalar.activation(out=wc, in_=wc, func=ACT.Ln)
+
+        def half_log(s):
+            log_wc = work[:, tiles_of(s), NC : 2 * NC]
+            nc.scalar.activation(
+                out=log_wc, in_=log_wc, func=ACT.Identity, bias=minus_one[:], scale=0.5
+            )
+
+        def variance(s):
+            var = out_pool.tile([P, UNIT, NC], F32, name="var")
+            yv = alive[("y", s)][1]
+            for lo, n, count in halves(s):
+                bank = psum.tile([P, 2, NC], F32, name="yv_rows", tag="to_vector")
+                for j in range(count):
+                    for block in range(2):
+                        nc.tensor.transpose(
+                            bank[:, j, block * P : (block + 1) * P],
+                            yv[:, block, (lo + j) * P : (lo + j + 1) * P],
+                            ident[:],
+                        )
+                nc.vector.scalar_tensor_tensor(
+                    out=var[:, lo : lo + count, :],
+                    in0=bank[:],
+                    scalar=2.0,
+                    in1=work[:, n : n + count, NC : 2 * NC],
+                    op0=ALU.min,
+                    op1=ALU.add,
+                )
+            nc.sync.dma_start(out=var_rows[:, tiles_of(s), :], in_=var[:])
+
+        def summands(s):
+            for lo, n, count in halves(s):
+                nc.vector.tensor_tensor(
+                    out=work[:, n : n + count, 0:NC], in0=work[:, n : n + count, NC : 2 * NC],
+                    in1=work[:, n : n + count, 0:NC], op=ALU.subtract,
+                )
+
+        def sum_over_g(s):
+            engine = nc.gpsimd if s + 1 < UNITS else nc.vector
+            sums = sum_pool.tile([P, UNIT, NC // 2], F32, name="sums")
+            alive[("sums", s)] = sums
+            for lo, n, count in halves(s):
+                pair = work[:, n : n + count, 0:NC].rearrange("p n (c g) -> p n c g", g=2)
+                engine.tensor_tensor(
+                    out=sums[:, lo : lo + count, :], in0=pair[:, :, :, 0], in1=pair[:, :, :, 1],
+                    op=ALU.add,
+                )
+
+        def log_scale(s):
+            sums = alive[("sums", s)]
+            scale = out_pool.tile([P, UNIT, NC // 2], F32, name="scale")
+            for lo, n, count in halves(s):
+                nc.vector.tensor_tensor(
+                    out=by_tile_and_i(scale[:, lo : lo + count, :]),
+                    in0=by_tile_and_i(sums[:, lo : lo + count, :]),
+                    in1=repeat_i(offset, n, count), op=ALU.add,
+                )
+            nc.sync.dma_start(out=scale_rows[:, tiles_of(s), :], in_=scale[:])
+
+        def logs(s):
+            if s == 0:
+                variance(s)
+            summands(s)
+            sum_over_g(s)
+            if s + 1 < UNITS:
+                variance(s + 1)
+            log_scale(s)
+
+        nc.scalar.activation(
+            out=as_njtg(half_inv_a), in_=repeat_t(svar), func=ACT.Exp, scale=-2.0
+        )
+        quantise_weights()
+        for s in range(-AHEAD_TRANSPOSE, AHEAD_FRONT):
+            front(s)
+            if s == -AHEAD_QUANTISE:
+                spread_state()
+        jobs = [(products, s) for s in range(UNITS)] + [(logs, s) for s in range(UNITS)]
+        for index, (job, s) in enumerate(jobs):
+            ahead = index + AHEAD_LN - UNITS
+            if 0 <= ahead < UNITS:
+                log_weight(ahead)
+            if 0 <= ahead - 1 < UNITS:
+                half_log(ahead - 1)
+            job(s)
+            if index + AHEAD_FRONT < UNITS:
+                front(index + AHEAD_FRONT)

@@ -22,14 +22,11 @@ ROWS = UNIT * P
 K = 512
 NC = 256
 NI = 8
-JTG = NC // NI
-JT = JTG // 2
-BLOCKS = 2 * NC // P
-AHEAD_PROJECT = 1
-AHEAD_QUANTISE = 2
-AHEAD_TRANSPOSE = 3
-AHEAD_FRONT = 2
-AHEAD_LN = 2
+JT = 16
+HALF = UNIT // 2
+BANKS_SCALAR = 4
+EARLY = 4
+SLOTS = 32
 
 
 def tile_chainlveg_pa_t_kernel(
@@ -43,142 +40,212 @@ def tile_chainlveg_pa_t_kernel(
 
     with ExitStack() as ctx:
         keep = ctx.enter_context(tc.tile_pool(name="keep", bufs=1))
+        x_pool = ctx.enter_context(tc.tile_pool(name="xs", bufs=4))
         grouped_pool = ctx.enter_context(tc.tile_pool(name="grouped", bufs=2))
         xq_pool = ctx.enter_context(tc.tile_pool(name="xq", bufs=3))
-        ym_pool = ctx.enter_context(tc.tile_pool(name="ym", bufs=2))
-        yv_pool = ctx.enter_context(tc.tile_pool(name="yv", bufs=UNITS))
-        da_pool = ctx.enter_context(tc.tile_pool(name="da", bufs=3))
+        wide_pool = ctx.enter_context(tc.tile_pool(name="wide", bufs=2))
+        am_pool = ctx.enter_context(tc.tile_pool(name="am", bufs=6))
+        row_pool = ctx.enter_context(tc.tile_pool(name="rows", bufs=3))
+        da_pool = ctx.enter_context(tc.tile_pool(name="da", bufs=2))
         out_pool = ctx.enter_context(tc.tile_pool(name="outs", bufs=3))
-        sum_pool = ctx.enter_context(tc.tile_pool(name="sums", bufs=2))
-        psum = ctx.enter_context(tc.psum_pool(name="psum", bufs=4))
+        psum_s = ctx.enter_context(tc.psum_pool(name="psum_s", bufs=BANKS_SCALAR))
+        psum_v = ctx.enter_context(tc.psum_pool(name="psum_v", bufs=8 - BANKS_SCALAR))
         ctx.enter_context(tc.manual_schedule())
 
         def tiles_of(s):
             return slice(s * UNIT, (s + 1) * UNIT)
 
-        x_sb = keep.tile([P, TILES, K], BF16, name="x_sb")
+        alive = {}
+
         w_raw = keep.tile([P, 4, 2 * NC], BF16, name="w_raw")
-        bias_rows = keep.tile([P, P], BF16, name="bias_rows")
+        bias_rows = keep.tile([P, NC], BF16, name="bias_rows")
         smu = keep.tile([P, TILES * 16], BF16, name="smu")
         svar = keep.tile([P, TILES * 16], BF16, name="svar")
         sw = keep.tile([P, TILES * 8], BF16, name="sw")
+        two = keep.tile([P, 1], F32, name="two")
+        nc.vector.memset(two[:], 2.0)
+        spare = keep.tile([P, 1], F32, name="spare")
+        nc.scalar.activation(out=spare[:], in_=two[:], func=ACT.Exp)
         nc.vector.memset(bias_rows[:], 0.0)
-        for w, first_column in ((tcm_w, 0), (tcv_w, NC)):
+
+        def load_x(s, pieces):
+            tile = x_pool.tile([P, UNIT, K], BF16, name="x_sb")
+            alive[("x", s)] = tile
+            step = UNIT // pieces
+            for lo in range(0, UNIT, step):
+                n = s * UNIT + lo
+                nc.sync.dma_start(out=tile[:, lo : lo + step, :], in_=x_rows[:, n : n + step, :])
+
+        def load_w(w, first_column):
             nc.sync.dma_start(
                 out=w_raw[:, :, first_column : first_column + NC],
                 in_=w.rearrange("(q t) c -> q t c", t=4),
             )
+
         nc.scalar.dma_start(
             out=svar[:], in_=s_var.rearrange("b (c n) j e g -> (b c) (n j e g)", n=TILES)
         )
-        nc.scalar.dma_start(out=x_sb[:, 0 : UNIT // 2, :], in_=x_rows[:, 0 : UNIT // 2, :])
-        nc.scalar.dma_start(out=x_sb[:, UNIT // 2 : UNIT, :], in_=x_rows[:, UNIT // 2 : UNIT, :])
-        nc.scalar.dma_start(out=bias_rows[0:2, :], in_=tcm_b.rearrange("(r c) -> r c", r=2))
-        nc.scalar.dma_start(out=bias_rows[2:4, :], in_=tcv_b.rearrange("(r c) -> r c", r=2))
-        nc.scalar.dma_start(
+        nc.scalar.dma_start(out=bias_rows[0:1, :], in_=tcm_b.rearrange("(r c) -> r c", r=1))
+        nc.scalar.dma_start(out=bias_rows[1:2, :], in_=tcv_b.rearrange("(r c) -> r c", r=1))
+        load_x(0, 2)
+        load_w(tcv_w, NC)
+        load_w(tcm_w, 0)
+        load_x(1, 1)
+        nc.sync.dma_start(
             out=smu[:], in_=s_mu.rearrange("b (c n) j e g -> (b c) (n j e g)", n=TILES)
         )
-        nc.sync.dma_start(out=x_sb[:, tiles_of(1), :], in_=x_rows[:, tiles_of(1), :])
-        nc.scalar.dma_start(
+        load_x(2, 1)
+        nc.sync.dma_start(
             out=sw[:], in_=s_weight.rearrange("b (c n) j e -> (b c) (n j e)", n=TILES)
         )
-        for s in range(2, UNITS):
-            nc.sync.dma_start(out=x_sb[:, tiles_of(s), :], in_=x_rows[:, tiles_of(s), :])
+        for s in range(3, 4):
+            load_x(s, 1)
 
         ident = keep.tile([P, P], F32, name="ident")
         masks.make_identity(nc, ident[:])
-        minus_one = keep.tile([P, 1], F32, name="minus_one")
-        nc.vector.memset(minus_one[:], -1.0)
-        w_grouped = keep.tile([P, 2 * NC, 4], BF16, name="w_grouped", align_bytes=64)
+        ident_bf16 = keep.tile([P, P], BF16, name="ident_bf16")
+        nc.gpsimd.tensor_copy(out=ident_bf16[:], in_=ident[:])
+        var_bias = keep.tile([P, 1], F32, name="var_bias")
+        nc.vector.memset(var_bias[:], 0.0)
+        nc.vector.tensor_scalar_add(
+            out=var_bias[:], in0=var_bias[:], scalar1=0.5 * math.log(2.0 * math.pi) - 1.0
+        )
+        packed = keep.tile([P, TILES, SLOTS], BF16, name="packed")
+        nc.vector.memset(packed[:], 0.0)
+        w_grouped = keep.tile([P, 2, 2, P, 4], BF16, name="w_grouped", align_bytes=64)
         w_codes = keep.tile([P, 2 * NC], U32, name="w_codes", align_bytes=64)
         w_scales = keep.tile([P, 2 * NC], U8, name="w_scales", align_bytes=64)
-        bias_f32 = keep.tile([P, P], F32, name="bias_f32")
-        bias_plus_1 = keep.tile([P, BLOCKS], F32, name="bias_plus_1")
-        work = keep.tile([P, TILES, 2 * NC], F32, name="work")
-        m1 = keep.tile([P, TILES, JTG], F32, name="m1")
-        m1_plus_1 = keep.tile([P, TILES, JTG], F32, name="m1_plus_1")
-        v1_plus_1 = keep.tile([P, TILES, JTG], F32, name="v1_plus_1")
-        half_inv_a = keep.tile([P, TILES, JTG], F32, name="half_inv_a")
-        v1_sum = keep.tile([P, TILES * 8], F32, name="v1_sum")
-        offset_j = keep.tile([P, TILES * 8], F32, name="offset_j")
-        offset = keep.tile([P, TILES, JT], F32, name="offset")
+        bias_f32 = keep.tile([P, 2, P], F32, name="bias_f32")
+        bias_m = keep.tile([P, 2], F32, name="bias_m")
+        bias_v = keep.tile([P, 2], F32, name="bias_v")
+        yv_all = keep.tile([P, UNITS, 2, ROWS], F32, name="yv_all")
+        wc_all = keep.tile([P, UNITS, 2, ROWS], F32, name="wc_all")
+        m1 = keep.tile([P, TILES, 2 * JT], F32, name="m1")
+        m1_plus_1 = keep.tile([P, TILES * 2, JT], F32, name="m1_plus_1")
+        half_inv_a = keep.tile([P, TILES * 2, JT], F32, name="half_inv_a")
+        two_v1 = keep.tile([P, TILES * 2, JT], BF16, name="two_v1")
+        packed_t = keep.tile([P, UNITS, P], BF16, name="packed_t")
+        picks = keep.tile([P, UNIT, 8], BF16, name="picks")
+        picks_v = keep.tile([P, UNIT, 8], BF16, name="picks_v")
+        select_offset = keep.tile([P, UNIT, P], BF16, name="select_offset")
+        sums = keep.tile([P, TILES, P], F32, name="sums")
 
-        alive = {}
-
-        def repeat_t(small):
-            return (
-                small[:]
-                .rearrange("p (a g) -> p a g", g=2)
-                .unsqueeze(2)
-                .to_broadcast([P, TILES * 8, 2, 2])
-            )
-
-        def as_njtg(full):
-            return full[:].rearrange("p n (j t g) -> p (n j) t g", t=2, g=2)
-
-        def by_i(ap):
-            return ap.rearrange("p (i c) -> p i c", i=NI)
-
-        def by_tile_and_i(ap):
-            return ap.rearrange("p n (i c) -> p n i c", i=NI)
-
-        def repeat_i(small, n, count):
-            width = small.shape[2]
-            return small[:, n : n + count, :].unsqueeze(2).to_broadcast([P, count, NI, width])
+        def spread(engine_op, out, small, **kw):
+            for g in range(2):
+                engine_op(
+                    out=out[:].rearrange("p (n g) (j t) -> p g n j t", g=2, t=2)[:, g],
+                    in0=small[:]
+                    .rearrange("p (n j g) -> p g n j", j=8, g=2)[:, g]
+                    .unsqueeze(3)
+                    .to_broadcast([P, TILES, 8, 2]),
+                    **kw,
+                )
 
         def halves(s):
-            return [(lo, s * UNIT + lo, UNIT // 2) for lo in range(0, UNIT, UNIT // 2)]
+            return [(lo, s * UNIT + lo) for lo in range(0, UNIT, HALF)]
 
-        def quantise_weights():
-            for first_column in (0, NC):
-                columns = slice(first_column, first_column + NC)
-                nc.vector.tensor_copy(
-                    out=w_grouped[:, columns, :],
-                    in_=w_raw[:, :, columns].rearrange("p t c -> p c t"),
-                )
-            for first_column in (0, NC):
-                columns = slice(first_column, first_column + NC)
-                nc.vector.quantize_mx(
-                    out=w_codes[:, columns].bitcast(FP8X4),
-                    scales=w_scales[:, columns],
-                    in_=w_grouped[:, columns, :].rearrange("p c t -> p (c t)"),
-                )
+        def wide(small, n, count):
+            return (
+                small[:, 2 * n : 2 * (n + count), :]
+                .unsqueeze(2)
+                .to_broadcast([P, 2 * count, NI, JT])
+            )
+
+        def by_ng(ap):
+            return ap.rearrange("p (a i c) -> p a i c", i=NI, c=JT)
+
+        def group_weights(which):
+            raw = w_raw[:, :, which * NC : (which + 1) * NC].rearrange(
+                "p t (c g) -> p g c t", g=2
+            )
+            for g in range(2):
+                nc.vector.tensor_copy(out=w_grouped[:, which, g, :, :], in_=raw[:, g])
+
+        def quantise_weights(which):
+            columns = slice(which * NC, (which + 1) * NC)
+            nc.vector.quantize_mx(
+                out=w_codes[:, columns].bitcast(FP8X4),
+                scales=w_scales[:, columns],
+                in_=w_grouped[:, which, :, :, :].rearrange("p g c t -> p (g c t)"),
+            )
 
         def bias_to_partitions():
-            nc.vector.tensor_copy(out=bias_f32[:], in_=bias_rows[:])
-            turned = psum.tile([P, 512], F32, name="turned", tag="to_scalar")
-            nc.tensor.transpose(turned[:, 0:P], bias_f32[:], ident[:])
-            nc.vector.tensor_scalar_add(
-                out=bias_plus_1[:], in0=turned[:, 0:BLOCKS], scalar1=1.0
-            )
-
-        def spread_state():
-            nc.vector.tensor_scalar_add(out=as_njtg(v1_plus_1), in0=repeat_t(svar), scalar1=1.0)
-            nc.vector.tensor_copy(out=as_njtg(m1), in_=repeat_t(smu))
-            nc.vector.tensor_scalar_add(out=m1_plus_1[:], in0=m1[:], scalar1=1.0)
-            nc.vector.tensor_scalar_mul(out=half_inv_a[:], in0=half_inv_a[:], scalar1=0.5)
-
-        def scale_offset():
-            pairs = svar[:].rearrange("p (a g) -> p a g", g=2)
-            nc.vector.tensor_tensor(
-                out=v1_sum[:], in0=pairs[:, :, 0], in1=pairs[:, :, 1], op=ALU.add
-            )
-            nc.vector.scalar_tensor_tensor(
-                out=offset_j[:], in0=sw[:], scalar=2.0 - math.log(2.0 * math.pi), in1=v1_sum[:],
-                op0=ALU.add, op1=ALU.subtract,
-            )
             nc.vector.tensor_copy(
-                out=offset[:].rearrange("p n (j t) -> p (n j) t", t=2),
-                in_=offset_j[:].unsqueeze(2).to_broadcast([P, TILES * 8, 2]),
+                out=bias_f32[:], in_=bias_rows[:].rearrange("p (c g) -> p g c", g=2)
             )
+            turned = psum_s.tile([P, 512], F32, name="turned", tag="to_scalar")
+            for g in range(2):
+                nc.tensor.transpose(turned[:, g * P : (g + 1) * P], bias_f32[:, g, :], ident[:])
+            by_row = turned[:, 0 : 2 * P].rearrange("p (g r) -> p r g", g=2)
+            nc.vector.tensor_scalar_add(out=bias_m[:], in0=by_row[:, 0, :], scalar1=1.0)
+            nc.vector.tensor_scalar(
+                out=bias_v[:], in0=by_row[:, 1, :], scalar1=2.0, scalar2=2.0,
+                op0=ALU.mult, op1=ALU.add,
+            )
+
+        def widen_var(s):
+            rows = slice(2 * s * UNIT, 2 * (s + 1) * UNIT)
+            wide_v1 = wide_pool.tile([P, 2 * UNIT, P], BF16, name="wide_v1")
+            alive[("wide", s)] = wide_v1
+            nc.vector.tensor_copy(
+                out=wide_v1[:].rearrange("p a (i c) -> p a i c", i=NI),
+                in_=two_v1[:, rows, :].unsqueeze(2).to_broadcast([P, 2 * UNIT, NI, JT]),
+            )
+
+        def spread_var():
+            spread(nc.vector.tensor_scalar, two_v1, svar, scalar1=2.0, scalar2=None, op0=ALU.mult)
+
+        def spread_mu():
+            spread(
+                nc.vector.tensor_scalar, m1_plus_1, smu, scalar1=1.0, scalar2=None, op0=ALU.add
+            )
+            nc.vector.tensor_scalar_mul(out=half_inv_a[:], in0=half_inv_a[:], scalar1=0.5)
+            nc.vector.tensor_copy(
+                out=m1[:].rearrange("p n (j t g) -> p (n j) t g", t=2, g=2),
+                in_=smu[:]
+                .rearrange("p (a g) -> p a g", g=2)
+                .unsqueeze(2)
+                .to_broadcast([P, TILES * 8, 2, 2]),
+            )
+
+        def offset_selector():
+            by_slot = ident_bf16[:].rearrange("p (n c) -> p n c", c=SLOTS)
+            nc.gpsimd.tensor_tensor(
+                out=picks_v[:], in0=by_slot[:, :, 8:24:2], in1=by_slot[:, :, 9:24:2], op=ALU.add
+            )
+            nc.gpsimd.tensor_tensor(
+                out=picks[:], in0=by_slot[:, :, 0:8], in1=picks_v[:], op=ALU.subtract
+            )
+            for lo in range(UNIT):
+                nc.gpsimd.tensor_scalar(
+                    out=select_offset[:, lo, :].rearrange("p (i j t) -> p i j t", i=NI, t=2),
+                    in0=picks[:, lo, :].unsqueeze(1).unsqueeze(3).to_broadcast([P, NI, 8, 2]),
+                    scalar1=2.0, scalar2=0.0, op0=ALU.mult, op1=ALU.add,
+                )
+
+        def pack_state():
+            nc.scalar.copy(
+                out=packed[:, :, 0:8], in_=sw[:].rearrange("p (n j) -> p n j", j=8)
+            )
+            nc.scalar.copy(
+                out=packed[:, :, 8:24], in_=svar[:].rearrange("p (n c) -> p n c", c=16)
+            )
+            turned = psum_s.tile([P, UNITS, P], BF16, name="packed_turned", tag="to_scalar")
+            for s in range(UNITS):
+                nc.tensor.transpose(
+                    turned[:, s, :],
+                    packed[:, tiles_of(s), :].rearrange("p n c -> p (n c)"),
+                    ident_bf16[:],
+                )
+            nc.scalar.copy(out=packed_t[:], in_=turned[:])
 
         def transpose_x(s):
             grouped = grouped_pool.tile([P, 4 * ROWS], BF16, name="grouped", align_bytes=64)
             alive[("grouped", s)] = grouped
             for lo in range(0, UNIT, 2):
-                turned = psum.tile([P, 2, 2 * P], F32, name="x_turned", tag="to_scalar")
+                turned = psum_s.tile([P, 2, 2 * P], F32, name="x_turned", tag="to_scalar")
                 for j in range(2):
-                    words = x_sb[:, s * UNIT + lo + j, :].bitcast(F32)
+                    words = alive[("x", s)][:, lo + j, :].bitcast(F32)
                     for u in range(2):
                         nc.tensor.transpose(
                             turned[:, u, j * P : (j + 1) * P],
@@ -200,194 +267,266 @@ def tile_chainlveg_pa_t_kernel(
                 out=codes[:].bitcast(FP8X4), scales=scales[:], in_=alive[("grouped", s)][:]
             )
 
-        def project(s):
+        def project(s, which):
             codes, scales = alive[("xq", s)]
-            y = (
-                ym_pool.tile([P, 2, ROWS], F32, name="ym"),
-                yv_pool.tile([P, 2, ROWS], F32, name="yv"),
-            )
-            alive[("y", s)] = y
-            for block in range(BLOCKS):
-                columns = slice(block * P, (block + 1) * P)
-                product = psum.tile([P, ROWS], F32, name="product", tag="to_scalar")
-                nc.tensor.matmul_mx(
-                    out=product[:],
-                    lhsT=w_codes[:, columns].bitcast(FP8X4),
-                    lhsT_scale=w_scales[:, columns],
-                    rhs=codes[:].bitcast(FP8X4),
-                    rhs_scale=scales[:],
-                    start=True,
-                    stop=True,
-                )
-                nc.scalar.activation(
-                    out=y[block // 2][:, block % 2, :], in_=product[:], func=ACT.Relu,
-                    bias=bias_plus_1[:, block : block + 1], scale=1.0,
-                )
-
-        def back_to_rows(s):
-            y = alive[("y", s)]
-            da = da_pool.tile([P, UNIT, NC], F32, name="da")
-            alive[("da", s)] = da
-            banks = []
-
-            def clip_and_subtract(lo, half, state_plus_1):
-                n = s * UNIT + lo
-                columns = slice(half * NC, (half + 1) * NC)
-                nc.vector.scalar_tensor_tensor(
-                    out=by_i(work[:, n, columns]),
-                    in0=by_i(banks[lo][:, columns]),
-                    scalar=2.0,
-                    in1=state_plus_1[:, n, :].unsqueeze(1).to_broadcast([P, NI, JTG]),
-                    op0=ALU.min,
-                    op1=ALU.subtract,
-                )
-
-            for lo in range(UNIT):
-                n = s * UNIT + lo
-                bank = psum.tile([P, 2 * NC], F32, name="y_rows", tag="to_vector")
-                banks.append(bank)
-                for block in range(BLOCKS):
-                    nc.tensor.transpose(
-                        bank[:, block * P : (block + 1) * P],
-                        y[block // 2][:, block % 2, lo * P : (lo + 1) * P],
-                        ident[:],
+            if which == 0:
+                alive[("am", s)] = am_pool.tile([P, 2, ROWS], F32, name="am")
+            for g in range(2):
+                if True:
+                    first = which * NC + g * P
+                    product = psum_s.tile([P, ROWS], F32, name="product", tag="to_scalar")
+                    nc.tensor.matmul_mx(
+                        out=product[:],
+                        lhsT=w_codes[:, first : first + P].bitcast(FP8X4),
+                        lhsT_scale=w_scales[:, first : first + P],
+                        rhs=codes[:].bitcast(FP8X4),
+                        rhs_scale=scales[:],
+                        start=True,
+                        stop=True,
                     )
-                clip_and_subtract(lo, 0, m1_plus_1)
-                nc.gpsimd.tensor_tensor(
-                    out=by_i(da[:, lo, :]),
-                    in0=by_i(work[:, n, 0:NC]),
-                    in1=half_inv_a[:, n, :].unsqueeze(1).to_broadcast([P, NI, JTG]),
-                    op=ALU.mult,
-                )
-            for lo in range(UNIT):
-                clip_and_subtract(lo, 1, v1_plus_1)
+                    if which == 1:
+                        nc.scalar.activation(
+                            out=yv_all[:, s, g, :], in_=product[:], func=ACT.Relu,
+                            bias=bias_v[:, g : g + 1], scale=2.0,
+                        )
+                    else:
+                        nc.scalar.activation(
+                            out=alive[("am", s)][:, g, :], in_=product[:], func=ACT.Relu,
+                            bias=bias_m[:, g : g + 1], scale=1.0,
+                        )
+
+        def turn_v1(s):
+            turned = psum_v.tile([P, 2, ROWS], BF16, name="v1_turned", tag="to_vector")
+            alive[("v1", s)] = turned
+            for g in range(2):
+                for lo in range(UNIT):
+                    nc.tensor.transpose(
+                        turned[:, g, lo * P : (lo + 1) * P],
+                        alive[("wide", s)][:, 2 * lo + g, :],
+                        ident_bf16[:],
+                    )
+
+        def difference(s):
+            nc.vector.scalar_tensor_tensor(
+                out=wc_all[:, s, :, :], in0=yv_all[:, s, :, :], scalar=4.0, in1=alive[("v1", s)][:],
+                op0=ALU.min, op1=ALU.subtract,
+            )
 
         def sigmoid(s):
-            u = work[:, tiles_of(s), NC : 2 * NC]
-            nc.scalar.activation(out=u, in_=u, func=ACT.Sigmoid, scale=-2.0)
-
-        def front(s):
-            if 0 <= s < UNITS:
-                back_to_rows(s)
-            if 0 <= s + AHEAD_QUANTISE < UNITS:
-                quantise_x(s + AHEAD_QUANTISE)
-            if s == 0:
-                scale_offset()
-            if 0 <= s + AHEAD_PROJECT < UNITS:
-                project(s + AHEAD_PROJECT)
-            if 0 <= s + AHEAD_TRANSPOSE < UNITS:
-                transpose_x(s + AHEAD_TRANSPOSE)
-                if s + AHEAD_TRANSPOSE == 0:
-                    bias_to_partitions()
-            if 0 <= s < UNITS:
-                sigmoid(s)
-
-        def products(s):
-            g = out_pool.tile([P, UNIT, NC], F32, name="g")
-            da = alive[("da", s)]
-            for lo, n, count in halves(s):
-                nc.vector.tensor_tensor(
-                    out=g[:, lo : lo + count, :], in0=work[:, n : n + count, 0:NC],
-                    in1=work[:, n : n + count, NC : 2 * NC], op=ALU.mult,
-                )
-            for lo, n, count in halves(s):
-                nc.vector.tensor_tensor(
-                    out=work[:, n : n + count, 0:NC], in0=g[:, lo : lo + count, :],
-                    in1=da[:, lo : lo + count, :], op=ALU.mult,
-                )
-            for lo, n, count in halves(s):
-                nc.vector.tensor_tensor(
-                    out=by_tile_and_i(g[:, lo : lo + count, :]),
-                    in0=by_tile_and_i(g[:, lo : lo + count, :]),
-                    in1=repeat_i(m1, n, count), op=ALU.add,
-                )
-            nc.sync.dma_start(out=mu_rows[:, tiles_of(s), :], in_=g[:])
-
-        def log_weight(s):
-            wc = work[:, tiles_of(s), NC : 2 * NC]
-            nc.scalar.activation(out=wc, in_=wc, func=ACT.Ln)
-
-        def half_log(s):
-            log_wc = work[:, tiles_of(s), NC : 2 * NC]
             nc.scalar.activation(
-                out=log_wc, in_=log_wc, func=ACT.Identity, bias=minus_one[:], scale=0.5
+                out=wc_all[:, s, :, :], in_=wc_all[:, s, :, :], func=ACT.Sigmoid, bias=two[:],
+                scale=-1.0,
             )
 
-        def variance(s):
-            var = out_pool.tile([P, UNIT, NC], F32, name="var")
-            yv = alive[("y", s)][1]
-            for lo, n, count in halves(s):
-                bank = psum.tile([P, 2, NC], F32, name="yv_rows", tag="to_vector")
-                for j in range(count):
-                    for block in range(2):
-                        nc.tensor.transpose(
-                            bank[:, j, block * P : (block + 1) * P],
-                            yv[:, block, (lo + j) * P : (lo + j + 1) * P],
-                            ident[:],
+        def clip_v(s):
+            nc.vector.tensor_scalar(
+                out=yv_all[:, s, :, :], in0=yv_all[:, s, :, :], scalar1=4.0, scalar2=None,
+                op0=ALU.min,
+            )
+
+        def to_rows(bank, source, lo):
+            for j in range(HALF):
+                for g in range(2):
+                    nc.tensor.transpose(
+                        bank[:, j, g, :], source[:, g, (lo + j) * P : (lo + j + 1) * P], ident[:]
+                    )
+
+        def turn_m(s):
+            for lo in range(0, UNIT, HALF):
+                bank = psum_v.tile([P, HALF, 2, P], F32, name="m_rows", tag="to_vector")
+                to_rows(bank, alive[("am", s)], lo)
+                alive[("m_rows", s, lo)] = bank
+
+        def sub_dn(s):
+            dn = row_pool.tile([P, UNIT * NC], F32, name="dn")
+            da = da_pool.tile([P, UNIT * NC], F32, name="da")
+            alive[("dn", s)] = dn
+            alive[("da", s)] = da
+            for lo, n in halves(s):
+                bank = alive[("m_rows", s, lo)]
+                part = slice(lo * NC, (lo + HALF) * NC)
+                for j in range(HALF):
+                    for g in range(2):
+                        first = ((lo + j) * 2 + g) * P
+                        nc.vector.scalar_tensor_tensor(
+                            out=dn[:, first : first + P].rearrange("p (i c) -> p i c", i=NI),
+                            in0=bank[:, j, g, :].rearrange("p (i c) -> p i c", i=NI),
+                            scalar=2.0,
+                            in1=m1_plus_1[:, 2 * (n + j) + g, :]
+                            .unsqueeze(1)
+                            .to_broadcast([P, NI, JT]),
+                            op0=ALU.min,
+                            op1=ALU.subtract,
                         )
-                nc.vector.scalar_tensor_tensor(
-                    out=var[:, lo : lo + count, :],
-                    in0=bank[:],
-                    scalar=2.0,
-                    in1=work[:, n : n + count, NC : 2 * NC],
-                    op0=ALU.min,
-                    op1=ALU.add,
+                nc.gpsimd.tensor_tensor(
+                    out=by_ng(da[:, part]), in0=by_ng(dn[:, part]), in1=wide(half_inv_a, n, HALF),
+                    op=ALU.mult,
+                )
+
+        def sub_product(s):
+            g_tile = row_pool.tile([P, UNIT * NC], F32, name="g_tile")
+            alive[("g", s)] = g_tile
+            for lo, n in halves(s):
+                bank = psum_v.tile([P, HALF, 2, P], F32, name="wc_rows", tag="to_vector")
+                to_rows(bank, wc_all[:, s, :, :], lo)
+                part = slice(lo * NC, (lo + HALF) * NC)
+                nc.vector.tensor_tensor(
+                    out=g_tile[:, part], in0=bank[:].rearrange("p n g c -> p (n g c)"),
+                    in1=alive[("dn", s)][:, part], op=ALU.mult,
+                )
+
+        def sub_square(s):
+            dn = alive[("dn", s)]
+            for lo, n in halves(s):
+                part = slice(lo * NC, (lo + HALF) * NC)
+                nc.vector.tensor_tensor(
+                    out=dn[:, part], in0=alive[("g", s)][:, part], in1=alive[("da", s)][:, part],
+                    op=ALU.mult,
+                )
+                q = dn[:, part].rearrange("p (n g c) -> p n g c", n=HALF, g=2)
+                nc.gpsimd.tensor_tensor(
+                    out=sums[:, n : n + HALF, :], in0=q[:, :, 0, :], in1=q[:, :, 1, :], op=ALU.add
+                )
+
+        def sub_mean(s):
+            mu = out_pool.tile([P, UNIT, NC], F32, name="mu", bufs=2)
+            for lo in range(UNIT):
+                g_rows = alive[("g", s)][:, lo * NC : (lo + 1) * NC].rearrange(
+                    "p (g i c) -> p i c g", g=2, i=NI
+                )
+                nc.vector.tensor_tensor(
+                    out=mu[:, lo, :].rearrange("p (i c g) -> p i c g", i=NI, g=2),
+                    in0=g_rows,
+                    in1=m1[:, s * UNIT + lo, :]
+                    .rearrange("p (c g) -> p c g", g=2)
+                    .unsqueeze(1)
+                    .to_broadcast([P, NI, JT, 2]),
+                    op=ALU.add,
+                )
+            nc.sync.dma_start(out=mu_rows[:, tiles_of(s), :], in_=mu[:])
+
+        def log_weight(s):
+            nc.scalar.activation(
+                out=wc_all[:, s, :, :], in_=wc_all[:, s, :, :], func=ACT.Ln,
+                scale=0.5 / math.pi,
+            )
+
+        def variance(s, on_vector=False):
+            var = out_pool.tile([P, UNIT, NC], F32, name="var")
+            for lo, n in halves(s):
+                bank = psum_s.tile([P, HALF, 2, P], F32, name="var_rows", tag="to_scalar")
+                for j in range(HALF):
+                    rows = slice((lo + j) * P, (lo + j + 1) * P)
+                    for g in range(2):
+                        nc.tensor.matmul(
+                            bank[:, j, g, :], lhsT=wc_all[:, s, g, rows], rhs=ident[:],
+                            is_transpose=True, start=True, stop=False,
+                        )
+                        nc.tensor.matmul(
+                            bank[:, j, g, :], lhsT=yv_all[:, s, g, rows], rhs=ident[:],
+                            is_transpose=True, start=False, stop=True,
+                        )
+                nc.scalar.activation(
+                    out=var[:, lo : lo + HALF, :].rearrange("p n (c g) -> p n c g", g=2),
+                    in_=bank[:].rearrange("p n g c -> p n c g"),
+                    func=ACT.Identity, bias=var_bias[:], scale=0.5,
                 )
             nc.sync.dma_start(out=var_rows[:, tiles_of(s), :], in_=var[:])
 
-        def summands(s):
-            for lo, n, count in halves(s):
-                nc.vector.tensor_tensor(
-                    out=work[:, n : n + count, 0:NC], in0=work[:, n : n + count, NC : 2 * NC],
-                    in1=work[:, n : n + count, 0:NC], op=ALU.subtract,
-                )
-
-        def sum_over_g(s):
-            engine = nc.gpsimd if s + 1 < UNITS else nc.vector
-            sums = sum_pool.tile([P, UNIT, NC // 2], F32, name="sums")
-            alive[("sums", s)] = sums
-            for lo, n, count in halves(s):
-                pair = work[:, n : n + count, 0:NC].rearrange("p n (c g) -> p n c g", g=2)
-                engine.tensor_tensor(
-                    out=sums[:, lo : lo + count, :], in0=pair[:, :, :, 0], in1=pair[:, :, :, 1],
-                    op=ALU.add,
-                )
-
         def log_scale(s):
-            sums = alive[("sums", s)]
-            scale = out_pool.tile([P, UNIT, NC // 2], F32, name="scale")
-            for lo, n, count in halves(s):
-                nc.vector.tensor_tensor(
-                    out=by_tile_and_i(scale[:, lo : lo + count, :]),
-                    in0=by_tile_and_i(sums[:, lo : lo + count, :]),
-                    in1=repeat_i(offset, n, count), op=ALU.add,
+            scale = out_pool.tile([P, UNIT, P], F32, name="scale")
+            bank = psum_v.tile([P, UNIT, P], F32, name="sum_rows", tag="to_vector")
+            for lo in range(UNIT):
+                rows = slice(lo * P, (lo + 1) * P)
+                nc.tensor.matmul(
+                    bank[:, lo, :], lhsT=packed_t[:, s, :], rhs=select_offset[:, lo, :],
+                    start=True, stop=False,
                 )
+                for g in range(2):
+                    nc.tensor.matmul(
+                        bank[:, lo, :], lhsT=wc_all[:, s, g, rows], rhs=ident[:],
+                        is_transpose=True, start=False, stop=(g == 1),
+                    )
+            nc.vector.scalar_tensor_tensor(
+                out=scale[:], in0=bank[:], scalar=0.5, in1=sums[:, tiles_of(s), :],
+                op0=ALU.mult, op1=ALU.subtract,
+            )
             nc.sync.dma_start(out=scale_rows[:, tiles_of(s), :], in_=scale[:])
 
-        def logs(s):
-            if s == 0:
-                variance(s)
-            summands(s)
-            sum_over_g(s)
+        for g in range(2):
+            nc.scalar.activation(
+                out=half_inv_a[:].rearrange("p (n g) (j t) -> p g n j t", g=2, t=2)[:, g],
+                in_=svar[:]
+                .rearrange("p (n j g) -> p g n j", j=8, g=2)[:, g]
+                .unsqueeze(3)
+                .to_broadcast([P, TILES, 8, 2]),
+                func=ACT.Exp, scale=-2.0,
+            )
+        nc.scalar.activation(out=spare[:], in_=two[:], func=ACT.Sigmoid)
+        spread_var()
+        widen_var(0)
+        transpose_x(0)
+        bias_to_partitions()
+        group_weights(1)
+        quantise_x(0)
+        quantise_weights(1)
+        project(0, 1)
+        turn_v1(0)
+        transpose_x(1)
+        group_weights(0)
+        quantise_weights(0)
+        project(0, 0)
+        widen_var(1)
+        quantise_x(1)
+        transpose_x(2)
+        offset_selector()
+        for s in range(UNITS):
+            u = (s - 1) // 2
+            if s + 4 < UNITS:
+                load_x(s + 4, 1)
+            if s % 2 == 1:
+                sub_dn(u)
+            elif s > 0:
+                sub_mean(u)
+                sub_square(u)
+            difference(s)
+            sigmoid(s)
+            if s % 2 == 1:
+                sub_product(u)
             if s + 1 < UNITS:
-                variance(s + 1)
-            log_scale(s)
-
-        nc.scalar.activation(
-            out=as_njtg(half_inv_a), in_=repeat_t(svar), func=ACT.Exp, scale=-2.0
-        )
-        quantise_weights()
-        for s in range(-AHEAD_TRANSPOSE, AHEAD_FRONT):
-            front(s)
-            if s == -AHEAD_QUANTISE:
-                spread_state()
-        jobs = [(products, s) for s in range(UNITS)] + [(logs, s) for s in range(UNITS)]
-        for index, (job, s) in enumerate(jobs):
-            ahead = index + AHEAD_LN - UNITS
-            if 0 <= ahead < UNITS:
-                log_weight(ahead)
-            if 0 <= ahead - 1 < UNITS:
-                half_log(ahead - 1)
-            job(s)
-            if index + AHEAD_FRONT < UNITS:
-                front(index + AHEAD_FRONT)
+                project(s + 1, 1)
+                project(s + 1, 0)
+                turn_v1(s + 1)
+            if s % 2 == 0:
+                turn_m(s // 2)
+            if s + 3 < UNITS:
+                transpose_x(s + 3)
+            if s == 0:
+                spread_mu()
+            clip_v(s)
+            if s + 2 < UNITS:
+                widen_var(s + 2)
+                quantise_x(s + 2)
+            if s == 1:
+                pack_state()
+        turn_m(EARLY)
+        sub_dn(EARLY)
+        sub_product(EARLY)
+        sub_mean(EARLY - 1)
+        sub_square(EARLY - 1)
+        for w in range(EARLY + 1):
+            log_weight(w)
+        ready = 0
+        for u in range(EARLY, UNITS):
+            if u + 1 < UNITS:
+                turn_m(u + 1)
+                sub_dn(u + 1)
+                sub_product(u + 1)
+                log_weight(u + 1)
+            variance(ready)
+            log_scale(ready)
+            sub_mean(u)
+            sub_square(u)
+            variance(ready + 1)
+            log_scale(ready + 1)
+            ready += 2

@@ -85,21 +85,20 @@ def tile_chainlveg_pa_t_kernel(
         nc.scalar.dma_start(
             out=svar[:], in_=s_var.rearrange("b (c n) j e g -> (b c) (n j e g)", n=TILES)
         )
+        load_x(0, 2)
         nc.scalar.dma_start(out=bias_rows[0:1, :], in_=tcm_b.rearrange("(r c) -> r c", r=1))
         nc.scalar.dma_start(out=bias_rows[1:2, :], in_=tcv_b.rearrange("(r c) -> r c", r=1))
-        load_x(0, 2)
+        nc.scalar.dma_start(
+            out=smu[:], in_=s_mu.rearrange("b (c n) j e g -> (b c) (n j e g)", n=TILES)
+        )
         load_w(tcv_w, NC)
         load_w(tcm_w, 0)
         load_x(1, 1)
-        nc.sync.dma_start(
-            out=smu[:], in_=s_mu.rearrange("b (c n) j e g -> (b c) (n j e g)", n=TILES)
-        )
         load_x(2, 1)
         nc.sync.dma_start(
             out=sw[:], in_=s_weight.rearrange("b (c n) j e -> (b c) (n j e)", n=TILES)
         )
-        for s in range(3, 4):
-            load_x(s, 1)
+        load_x(3, 1)
 
         ident = keep.tile([P, P], F32, name="ident")
         masks.make_identity(nc, ident[:])
@@ -467,6 +466,7 @@ def tile_chainlveg_pa_t_kernel(
         widen_var(0)
         transpose_x(0)
         bias_to_partitions()
+        widen_var(1)
         group_weights(1)
         quantise_x(0)
         quantise_weights(1)
@@ -476,7 +476,7 @@ def tile_chainlveg_pa_t_kernel(
         group_weights(0)
         quantise_weights(0)
         project(0, 0)
-        widen_var(1)
+        spread_mu()
         quantise_x(1)
         transpose_x(2)
         offset_selector()
@@ -495,14 +495,13 @@ def tile_chainlveg_pa_t_kernel(
                 sub_product(u)
             if s + 1 < UNITS:
                 project(s + 1, 1)
-                project(s + 1, 0)
                 turn_v1(s + 1)
             if s % 2 == 0:
                 turn_m(s // 2)
             if s + 3 < UNITS:
                 transpose_x(s + 3)
-            if s == 0:
-                spread_mu()
+            if s + 1 < UNITS:
+                project(s + 1, 0)
             clip_v(s)
             if s + 2 < UNITS:
                 widen_var(s + 2)

@@ -22,7 +22,8 @@ ROWS = UNIT * P
 K = 512
 NC = 256
 NI = 8
-JT = 16
+JTG = NC // NI
+JT = JTG // 2
 HALF = UNIT // 2
 BANKS_SCALAR = 4
 EARLY = 4
@@ -119,9 +120,9 @@ def tile_chainlveg_pa_t_kernel(
         bias_v = keep.tile([P, 2], F32, name="bias_v")
         yv_all = keep.tile([P, UNITS, 2, ROWS], F32, name="yv_all")
         wc_all = keep.tile([P, UNITS, 2, ROWS], F32, name="wc_all")
-        m1 = keep.tile([P, TILES, 2 * JT], F32, name="m1")
-        m1_plus_1 = keep.tile([P, TILES * 2, JT], F32, name="m1_plus_1")
-        half_inv_a = keep.tile([P, TILES * 2, JT], F32, name="half_inv_a")
+        m1 = keep.tile([P, TILES, JTG], BF16, name="m1")
+        m1_plus_1 = keep.tile([P, TILES, JTG], F32, name="m1_plus_1")
+        half_inv_a = keep.tile([P, TILES, JTG], F32, name="half_inv_a")
         two_v1 = keep.tile([P, TILES * 2, JT], BF16, name="two_v1")
         packed_t = keep.tile([P, UNITS, P], BF16, name="packed_t")
         picks = keep.tile([P, UNIT, 8], BF16, name="picks")
@@ -143,15 +144,22 @@ def tile_chainlveg_pa_t_kernel(
         def halves(s):
             return [(lo, s * UNIT + lo) for lo in range(0, UNIT, HALF)]
 
-        def wide(small, n, count):
+        def repeat_t(small):
             return (
-                small[:, 2 * n : 2 * (n + count), :]
+                small[:]
+                .rearrange("p (a g) -> p a g", g=2)
                 .unsqueeze(2)
-                .to_broadcast([P, 2 * count, NI, JT])
+                .to_broadcast([P, TILES * 8, 2, 2])
             )
 
-        def by_ng(ap):
-            return ap.rearrange("p (a i c) -> p a i c", i=NI, c=JT)
+        def as_njtg(full):
+            return full[:].rearrange("p n (j t g) -> p (n j) t g", t=2, g=2)
+
+        def repeat_i(small, n, count):
+            return small[:, n : n + count, :].unsqueeze(2).to_broadcast([P, count, NI, JTG])
+
+        def by_tile_and_i(ap, count):
+            return ap.rearrange("p (n i c) -> p n i c", n=count, i=NI)
 
         def group_weights(which):
             raw = w_raw[:, :, which * NC : (which + 1) * NC].rearrange(
@@ -195,17 +203,9 @@ def tile_chainlveg_pa_t_kernel(
             spread(nc.vector.tensor_scalar, two_v1, svar, scalar1=2.0, scalar2=None, op0=ALU.mult)
 
         def spread_mu():
-            spread(
-                nc.vector.tensor_scalar, m1_plus_1, smu, scalar1=1.0, scalar2=None, op0=ALU.add
-            )
+            nc.vector.tensor_copy(out=as_njtg(m1), in_=repeat_t(smu))
+            nc.vector.tensor_scalar_add(out=m1_plus_1[:], in0=m1[:], scalar1=1.0)
             nc.vector.tensor_scalar_mul(out=half_inv_a[:], in0=half_inv_a[:], scalar1=0.5)
-            nc.vector.tensor_copy(
-                out=m1[:].rearrange("p n (j t g) -> p (n j) t g", t=2, g=2),
-                in_=smu[:]
-                .rearrange("p (a g) -> p a g", g=2)
-                .unsqueeze(2)
-                .to_broadcast([P, TILES * 8, 2, 2]),
-            )
 
         def offset_selector():
             by_slot = ident_bf16[:].rearrange("p (n c) -> p n c", c=SLOTS)
@@ -345,21 +345,22 @@ def tile_chainlveg_pa_t_kernel(
                 bank = alive[("m_rows", s, lo)]
                 part = slice(lo * NC, (lo + HALF) * NC)
                 for j in range(HALF):
-                    for g in range(2):
-                        first = ((lo + j) * 2 + g) * P
-                        nc.vector.scalar_tensor_tensor(
-                            out=dn[:, first : first + P].rearrange("p (i c) -> p i c", i=NI),
-                            in0=bank[:, j, g, :].rearrange("p (i c) -> p i c", i=NI),
-                            scalar=2.0,
-                            in1=m1_plus_1[:, 2 * (n + j) + g, :]
-                            .unsqueeze(1)
-                            .to_broadcast([P, NI, JT]),
-                            op0=ALU.min,
-                            op1=ALU.subtract,
-                        )
+                    nc.vector.scalar_tensor_tensor(
+                        out=dn[:, (lo + j) * NC : (lo + j + 1) * NC].rearrange(
+                            "p (i c g) -> p i c g", i=NI, g=2
+                        ),
+                        in0=bank[:, j, :, :].rearrange("p g (i c) -> p i c g", i=NI),
+                        scalar=2.0,
+                        in1=m1_plus_1[:, n + j, :]
+                        .rearrange("p (c g) -> p c g", g=2)
+                        .unsqueeze(1)
+                        .to_broadcast([P, NI, JT, 2]),
+                        op0=ALU.min,
+                        op1=ALU.subtract,
+                    )
                 nc.gpsimd.tensor_tensor(
-                    out=by_ng(da[:, part]), in0=by_ng(dn[:, part]), in1=wide(half_inv_a, n, HALF),
-                    op=ALU.mult,
+                    out=by_tile_and_i(da[:, part], HALF), in0=by_tile_and_i(dn[:, part], HALF),
+                    in1=repeat_i(half_inv_a, n, HALF), op=ALU.mult,
                 )
 
         def sub_product(s):
@@ -370,39 +371,31 @@ def tile_chainlveg_pa_t_kernel(
                 to_rows(bank, wc_all[:, s, :, :], lo)
                 part = slice(lo * NC, (lo + HALF) * NC)
                 nc.vector.tensor_tensor(
-                    out=g_tile[:, part], in0=bank[:].rearrange("p n g c -> p (n g c)"),
-                    in1=alive[("dn", s)][:, part], op=ALU.mult,
+                    out=g_tile[:, part].rearrange("p (n c g) -> p n c g", n=HALF, g=2),
+                    in0=bank[:].rearrange("p n g c -> p n c g"),
+                    in1=alive[("dn", s)][:, part].rearrange("p (n c g) -> p n c g", n=HALF, g=2),
+                    op=ALU.mult,
                 )
 
         def sub_square(s):
             dn = alive[("dn", s)]
-            for lo, n in halves(s):
-                part = slice(lo * NC, (lo + HALF) * NC)
-                nc.vector.tensor_tensor(
-                    out=dn[:, part], in0=alive[("g", s)][:, part], in1=alive[("da", s)][:, part],
-                    op=ALU.mult,
-                )
-                q = dn[:, part].rearrange("p (n g c) -> p n g c", n=HALF, g=2)
-                nc.gpsimd.tensor_tensor(
-                    out=sums[:, n : n + HALF, :], in0=q[:, :, 0, :], in1=q[:, :, 1, :], op=ALU.add
-                )
+            nc.vector.tensor_tensor(
+                out=dn[:], in0=alive[("g", s)][:], in1=alive[("da", s)][:], op=ALU.mult
+            )
+            pair = dn[:].rearrange("p (n c g) -> p n c g", n=UNIT, g=2)
+            nc.gpsimd.tensor_tensor(
+                out=sums[:, tiles_of(s), :], in0=pair[:, :, :, 0], in1=pair[:, :, :, 1], op=ALU.add
+            )
 
         def sub_mean(s):
-            mu = out_pool.tile([P, UNIT, NC], F32, name="mu", bufs=2)
-            for lo in range(UNIT):
-                g_rows = alive[("g", s)][:, lo * NC : (lo + 1) * NC].rearrange(
-                    "p (g i c) -> p i c g", g=2, i=NI
-                )
-                nc.vector.tensor_tensor(
-                    out=mu[:, lo, :].rearrange("p (i c g) -> p i c g", i=NI, g=2),
-                    in0=g_rows,
-                    in1=m1[:, s * UNIT + lo, :]
-                    .rearrange("p (c g) -> p c g", g=2)
-                    .unsqueeze(1)
-                    .to_broadcast([P, NI, JT, 2]),
-                    op=ALU.add,
-                )
-            nc.sync.dma_start(out=mu_rows[:, tiles_of(s), :], in_=mu[:])
+            mu = out_pool.tile([P, UNIT * NC], F32, name="mu", bufs=2)
+            nc.vector.tensor_tensor(
+                out=by_tile_and_i(mu[:], UNIT), in0=by_tile_and_i(alive[("g", s)][:], UNIT),
+                in1=repeat_i(m1, s * UNIT, UNIT), op=ALU.add,
+            )
+            nc.sync.dma_start(
+                out=mu_rows[:, tiles_of(s), :], in_=mu[:].rearrange("p (n c) -> p n c", n=UNIT)
+            )
 
         def log_weight(s):
             nc.scalar.activation(
@@ -452,15 +445,9 @@ def tile_chainlveg_pa_t_kernel(
             )
             nc.sync.dma_start(out=scale_rows[:, tiles_of(s), :], in_=scale[:])
 
-        for g in range(2):
-            nc.scalar.activation(
-                out=half_inv_a[:].rearrange("p (n g) (j t) -> p g n j t", g=2, t=2)[:, g],
-                in_=svar[:]
-                .rearrange("p (n j g) -> p g n j", j=8, g=2)[:, g]
-                .unsqueeze(3)
-                .to_broadcast([P, TILES, 8, 2]),
-                func=ACT.Exp, scale=-2.0,
-            )
+        nc.scalar.activation(
+            out=as_njtg(half_inv_a), in_=repeat_t(svar), func=ACT.Exp, scale=-2.0
+        )
         nc.scalar.activation(out=spare[:], in_=two[:], func=ACT.Sigmoid)
         spread_var()
         widen_var(0)

@@ -27,6 +27,7 @@ JT = JTG // 2
 HALF = UNIT // 2
 BANKS_SCALAR = 4
 EARLY = 4
+ADDED_FROM = 7
 SLOTS = 32
 
 
@@ -86,19 +87,19 @@ def tile_chainlveg_pa_t_kernel(
         nc.scalar.dma_start(
             out=svar[:], in_=s_var.rearrange("b (c n) j e g -> (b c) (n j e g)", n=TILES)
         )
-        load_x(0, 2)
         nc.scalar.dma_start(out=bias_rows[0:1, :], in_=tcm_b.rearrange("(r c) -> r c", r=1))
         nc.scalar.dma_start(out=bias_rows[1:2, :], in_=tcv_b.rearrange("(r c) -> r c", r=1))
+        load_x(0, 2)
+        load_w(tcv_w, NC)
         nc.scalar.dma_start(
             out=smu[:], in_=s_mu.rearrange("b (c n) j e g -> (b c) (n j e g)", n=TILES)
         )
-        load_w(tcv_w, NC)
         load_w(tcm_w, 0)
-        load_x(1, 1)
-        load_x(2, 1)
         nc.sync.dma_start(
             out=sw[:], in_=s_weight.rearrange("b (c n) j e -> (b c) (n j e)", n=TILES)
         )
+        load_x(1, 1)
+        load_x(2, 1)
         load_x(3, 1)
 
         ident = keep.tile([P, P], F32, name="ident")
@@ -229,6 +230,8 @@ def tile_chainlveg_pa_t_kernel(
             nc.scalar.copy(
                 out=packed[:, :, 8:24], in_=svar[:].rearrange("p (n c) -> p n c", c=16)
             )
+
+        def turn_state():
             turned = psum_s.tile([P, UNITS, P], BF16, name="packed_turned", tag="to_scalar")
             for s in range(UNITS):
                 nc.tensor.transpose(
@@ -317,6 +320,12 @@ def tile_chainlveg_pa_t_kernel(
                 scale=-1.0,
             )
 
+        def clip_and_add(s):
+            nc.vector.scalar_tensor_tensor(
+                out=yv_all[:, s, :, :], in0=yv_all[:, s, :, :], scalar=4.0,
+                in1=wc_all[:, s, :, :], op0=ALU.min, op1=ALU.add,
+            )
+
         def clip_v(s):
             nc.vector.tensor_scalar(
                 out=yv_all[:, s, :, :], in0=yv_all[:, s, :, :], scalar1=4.0, scalar2=None,
@@ -363,12 +372,17 @@ def tile_chainlveg_pa_t_kernel(
                     in1=repeat_i(half_inv_a, n, HALF), op=ALU.mult,
                 )
 
+        def turn_wc(s):
+            for lo in range(0, UNIT, HALF):
+                bank = psum_v.tile([P, HALF, 2, P], F32, name="wc_rows", tag="to_vector")
+                to_rows(bank, wc_all[:, s, :, :], lo)
+                alive[("wc_rows", s, lo)] = bank
+
         def sub_product(s):
             g_tile = row_pool.tile([P, UNIT * NC], F32, name="g_tile")
             alive[("g", s)] = g_tile
             for lo, n in halves(s):
-                bank = psum_v.tile([P, HALF, 2, P], F32, name="wc_rows", tag="to_vector")
-                to_rows(bank, wc_all[:, s, :, :], lo)
+                bank = alive[("wc_rows", s, lo)]
                 part = slice(lo * NC, (lo + HALF) * NC)
                 nc.vector.tensor_tensor(
                     out=g_tile[:, part].rearrange("p (n c g) -> p n c g", n=HALF, g=2),
@@ -410,6 +424,11 @@ def tile_chainlveg_pa_t_kernel(
                 for j in range(HALF):
                     rows = slice((lo + j) * P, (lo + j + 1) * P)
                     for g in range(2):
+                        if s >= ADDED_FROM:
+                            nc.tensor.transpose(
+                                bank[:, j, g, :], yv_all[:, s, g, rows], ident[:]
+                            )
+                            continue
                         nc.tensor.matmul(
                             bank[:, j, g, :], lhsT=wc_all[:, s, g, rows], rhs=ident[:],
                             is_transpose=True, start=True, stop=False,
@@ -425,9 +444,9 @@ def tile_chainlveg_pa_t_kernel(
                 )
             nc.sync.dma_start(out=var_rows[:, tiles_of(s), :], in_=var[:])
 
-        def log_scale(s):
-            scale = out_pool.tile([P, UNIT, P], F32, name="scale")
+        def sum_logs(s):
             bank = psum_v.tile([P, UNIT, P], F32, name="sum_rows", tag="to_vector")
+            alive[("sum_rows", s)] = bank
             for lo in range(UNIT):
                 rows = slice(lo * P, (lo + 1) * P)
                 nc.tensor.matmul(
@@ -439,6 +458,10 @@ def tile_chainlveg_pa_t_kernel(
                         bank[:, lo, :], lhsT=wc_all[:, s, g, rows], rhs=ident[:],
                         is_transpose=True, start=False, stop=(g == 1),
                     )
+
+        def log_scale(s):
+            scale = out_pool.tile([P, UNIT, P], F32, name="scale")
+            bank = alive[("sum_rows", s)]
             nc.vector.scalar_tensor_tensor(
                 out=scale[:], in0=bank[:], scalar=0.5, in1=sums[:, tiles_of(s), :],
                 op0=ALU.mult, op1=ALU.subtract,
@@ -448,71 +471,78 @@ def tile_chainlveg_pa_t_kernel(
         nc.scalar.activation(
             out=as_njtg(half_inv_a), in_=repeat_t(svar), func=ACT.Exp, scale=-2.0
         )
-        nc.scalar.activation(out=spare[:], in_=two[:], func=ACT.Sigmoid)
+        offset_selector()
         spread_var()
         widen_var(0)
         transpose_x(0)
+        nc.scalar.activation(out=spare[:], in_=two[:], func=ACT.Sigmoid)
         bias_to_partitions()
-        widen_var(1)
         group_weights(1)
         quantise_x(0)
         quantise_weights(1)
-        project(0, 1)
-        turn_v1(0)
-        transpose_x(1)
+        pack_state()
+        widen_var(1)
         group_weights(0)
         quantise_weights(0)
-        project(0, 0)
-        spread_mu()
-        quantise_x(1)
-        transpose_x(2)
-        offset_selector()
         for s in range(UNITS):
             u = (s - 1) // 2
-            if s + 4 < UNITS:
-                load_x(s + 4, 1)
+            if 4 <= s + 3 < UNITS:
+                load_x(s + 3, 1)
+            project(s, 1)
+            if s % 2 == 1:
+                turn_wc(u)
+            turn_v1(s)
+            if s == 0:
+                transpose_x(1)
+                spread_mu()
+            project(s, 0)
+            if s + 2 < UNITS:
+                transpose_x(s + 2)
+            if s == 1:
+                turn_state()
             if s % 2 == 1:
                 sub_dn(u)
+                sub_product(u)
             elif s > 0:
                 sub_mean(u)
                 sub_square(u)
             difference(s)
             sigmoid(s)
-            if s % 2 == 1:
-                sub_product(u)
-            if s + 1 < UNITS:
-                project(s + 1, 1)
-                turn_v1(s + 1)
             if s % 2 == 0:
                 turn_m(s // 2)
-            if s + 3 < UNITS:
-                transpose_x(s + 3)
             if s + 1 < UNITS:
-                project(s + 1, 0)
-            clip_v(s)
+                quantise_x(s + 1)
+            if s < ADDED_FROM:
+                clip_v(s)
             if s + 2 < UNITS:
                 widen_var(s + 2)
-                quantise_x(s + 2)
-            if s == 1:
-                pack_state()
         turn_m(EARLY)
+        for w in range(EARLY):
+            log_weight(w)
         sub_dn(EARLY)
+        turn_wc(EARLY)
         sub_product(EARLY)
+        log_weight(EARLY)
         sub_mean(EARLY - 1)
         sub_square(EARLY - 1)
-        for w in range(EARLY + 1):
-            log_weight(w)
         ready = 0
         for u in range(EARLY, UNITS):
             if u + 1 < UNITS:
                 turn_m(u + 1)
+                turn_wc(u + 1)
                 sub_dn(u + 1)
                 sub_product(u + 1)
                 log_weight(u + 1)
+            if ready >= ADDED_FROM:
+                clip_and_add(ready)
             variance(ready)
-            log_scale(ready)
+            sum_logs(ready)
             sub_mean(u)
+            if ready + 1 >= ADDED_FROM:
+                clip_and_add(ready + 1)
             sub_square(u)
+            log_scale(ready)
             variance(ready + 1)
+            sum_logs(ready + 1)
             log_scale(ready + 1)
             ready += 2

@@ -27,6 +27,7 @@ JT = JTG // 2
 HALF = UNIT // 2
 BANKS_SCALAR = 4
 EARLY = 4
+VAR_BIAS = 0.5 * math.log(2.0 * math.pi) - 1.0
 ADDED_FROM = 7
 SLOTS = 32
 
@@ -106,11 +107,6 @@ def tile_chainlveg_pa_t_kernel(
         masks.make_identity(nc, ident[:])
         ident_bf16 = keep.tile([P, P], BF16, name="ident_bf16")
         nc.gpsimd.tensor_copy(out=ident_bf16[:], in_=ident[:])
-        var_bias = keep.tile([P, 1], F32, name="var_bias")
-        nc.vector.memset(var_bias[:], 0.0)
-        nc.vector.tensor_scalar_add(
-            out=var_bias[:], in0=var_bias[:], scalar1=0.5 * math.log(2.0 * math.pi) - 1.0
-        )
         packed = keep.tile([P, TILES, SLOTS], BF16, name="packed")
         nc.vector.memset(packed[:], 0.0)
         w_grouped = keep.tile([P, 2, 2, P, 4], BF16, name="w_grouped", align_bytes=64)
@@ -124,23 +120,12 @@ def tile_chainlveg_pa_t_kernel(
         m1 = keep.tile([P, TILES, JTG], BF16, name="m1")
         m1_plus_1 = keep.tile([P, TILES, JTG], F32, name="m1_plus_1")
         half_inv_a = keep.tile([P, TILES, JTG], F32, name="half_inv_a")
-        two_v1 = keep.tile([P, TILES * 2, JT], BF16, name="two_v1")
+        two_v1 = keep.tile([P, TILES, JTG], BF16, name="two_v1")
         packed_t = keep.tile([P, UNITS, P], BF16, name="packed_t")
         picks = keep.tile([P, UNIT, 8], BF16, name="picks")
         picks_v = keep.tile([P, UNIT, 8], BF16, name="picks_v")
         select_offset = keep.tile([P, UNIT, P], BF16, name="select_offset")
         sums = keep.tile([P, TILES, P], F32, name="sums")
-
-        def spread(engine_op, out, small, **kw):
-            for g in range(2):
-                engine_op(
-                    out=out[:].rearrange("p (n g) (j t) -> p g n j t", g=2, t=2)[:, g],
-                    in0=small[:]
-                    .rearrange("p (n j g) -> p g n j", j=8, g=2)[:, g]
-                    .unsqueeze(3)
-                    .to_broadcast([P, TILES, 8, 2]),
-                    **kw,
-                )
 
         def halves(s):
             return [(lo, s * UNIT + lo) for lo in range(0, UNIT, HALF)]
@@ -192,16 +177,17 @@ def tile_chainlveg_pa_t_kernel(
             )
 
         def widen_var(s):
-            rows = slice(2 * s * UNIT, 2 * (s + 1) * UNIT)
-            wide_v1 = wide_pool.tile([P, 2 * UNIT, P], BF16, name="wide_v1")
+            wide_v1 = wide_pool.tile([P, UNIT, NC], BF16, name="wide_v1")
             alive[("wide", s)] = wide_v1
             nc.vector.tensor_copy(
-                out=wide_v1[:].rearrange("p a (i c) -> p a i c", i=NI),
-                in_=two_v1[:, rows, :].unsqueeze(2).to_broadcast([P, 2 * UNIT, NI, JT]),
+                out=wide_v1[:].rearrange("p n (i c) -> p n i c", i=NI),
+                in_=two_v1[:, tiles_of(s), :].unsqueeze(2).to_broadcast([P, UNIT, NI, JTG]),
             )
 
         def spread_var():
-            spread(nc.vector.tensor_scalar, two_v1, svar, scalar1=2.0, scalar2=None, op0=ALU.mult)
+            nc.vector.tensor_scalar(
+                out=as_njtg(two_v1), in0=repeat_t(svar), scalar1=2.0, scalar2=None, op0=ALU.mult
+            )
 
         def spread_mu():
             nc.vector.tensor_copy(out=as_njtg(m1), in_=repeat_t(smu))
@@ -298,19 +284,18 @@ def tile_chainlveg_pa_t_kernel(
                         )
 
         def turn_v1(s):
-            turned = psum_v.tile([P, 2, ROWS], BF16, name="v1_turned", tag="to_vector")
+            turned = psum_v.tile([P, ROWS], F32, name="v1_turned", tag="to_vector")
             alive[("v1", s)] = turned
-            for g in range(2):
-                for lo in range(UNIT):
-                    nc.tensor.transpose(
-                        turned[:, g, lo * P : (lo + 1) * P],
-                        alive[("wide", s)][:, 2 * lo + g, :],
-                        ident_bf16[:],
-                    )
+            for lo in range(UNIT):
+                nc.tensor.transpose(
+                    turned[:, lo * P : (lo + 1) * P],
+                    alive[("wide", s)][:, lo, :].bitcast(F32),
+                    ident[:],
+                )
 
         def difference(s):
             nc.vector.scalar_tensor_tensor(
-                out=wc_all[:, s, :, :], in0=yv_all[:, s, :, :], scalar=4.0, in1=alive[("v1", s)][:],
+                out=wc_all[:, s, :, :], in0=yv_all[:, s, :, :], scalar=4.0, in1=alive[("v1", s)][:].bitcast(BF16).rearrange("p (r g) -> p g r", g=2),
                 op0=ALU.min, op1=ALU.subtract,
             )
 
@@ -440,7 +425,7 @@ def tile_chainlveg_pa_t_kernel(
                 nc.scalar.activation(
                     out=var[:, lo : lo + HALF, :].rearrange("p n (c g) -> p n c g", g=2),
                     in_=bank[:].rearrange("p n g c -> p n c g"),
-                    func=ACT.Identity, bias=var_bias[:], scale=0.5,
+                    func=ACT.Copy, bias=VAR_BIAS, scale=0.5,
                 )
             nc.sync.dma_start(out=var_rows[:, tiles_of(s), :], in_=var[:])
 

@@ -45,7 +45,7 @@ def tile_chainlveg_pa_t_kernel(
         keep = ctx.enter_context(tc.tile_pool(name="keep", bufs=1))
         x_pool = ctx.enter_context(tc.tile_pool(name="xs", bufs=4))
         grouped_pool = ctx.enter_context(tc.tile_pool(name="grouped", bufs=2))
-        xq_pool = ctx.enter_context(tc.tile_pool(name="xq", bufs=3))
+        xq_pool = ctx.enter_context(tc.tile_pool(name="xq", bufs=4))
         wide_pool = ctx.enter_context(tc.tile_pool(name="wide", bufs=2))
         am_pool = ctx.enter_context(tc.tile_pool(name="am", bufs=6))
         row_pool = ctx.enter_context(tc.tile_pool(name="rows", bufs=3))
@@ -169,6 +169,10 @@ def tile_chainlveg_pa_t_kernel(
             turned = psum_s.tile([P, 512], F32, name="turned", tag="to_scalar")
             for g in range(2):
                 nc.tensor.transpose(turned[:, g * P : (g + 1) * P], bias_f32[:, g, :], ident[:])
+            alive["bias_rows"] = turned
+
+        def bias_offsets():
+            turned = alive["bias_rows"]
             by_row = turned[:, 0 : 2 * P].rearrange("p (g r) -> p r g", g=2)
             nc.vector.tensor_scalar_add(out=bias_m[:], in0=by_row[:, 0, :], scalar1=1.0)
             nc.vector.tensor_scalar(
@@ -176,12 +180,14 @@ def tile_chainlveg_pa_t_kernel(
                 op0=ALU.mult, op1=ALU.add,
             )
 
-        def widen_var(s):
-            wide_v1 = wide_pool.tile([P, UNIT, NC], BF16, name="wide_v1")
-            alive[("wide", s)] = wide_v1
+        def widen_var(first, units):
+            wide_v1 = wide_pool.tile([P, units * UNIT, NC], BF16, name="wide_v1")
+            for s in range(units):
+                alive[("wide", first + s)] = wide_v1[:, tiles_of(s), :]
+            rows = slice(first * UNIT, (first + units) * UNIT)
             nc.vector.tensor_copy(
                 out=wide_v1[:].rearrange("p n (i c) -> p n i c", i=NI),
-                in_=two_v1[:, tiles_of(s), :].unsqueeze(2).to_broadcast([P, UNIT, NI, JTG]),
+                in_=two_v1[:, rows, :].unsqueeze(2).to_broadcast([P, units * UNIT, NI, JTG]),
             )
 
         def spread_var():
@@ -192,7 +198,6 @@ def tile_chainlveg_pa_t_kernel(
         def spread_mu():
             nc.vector.tensor_copy(out=as_njtg(m1), in_=repeat_t(smu))
             nc.vector.tensor_scalar_add(out=m1_plus_1[:], in0=m1[:], scalar1=1.0)
-            nc.vector.tensor_scalar_mul(out=half_inv_a[:], in0=half_inv_a[:], scalar1=0.5)
 
         def offset_selector():
             by_slot = ident_bf16[:].rearrange("p (n c) -> p n c", c=SLOTS)
@@ -311,10 +316,10 @@ def tile_chainlveg_pa_t_kernel(
                 in1=wc_all[:, s, :, :], op0=ALU.min, op1=ALU.add,
             )
 
-        def clip_v(s):
+        def clip_v(first, last):
             nc.vector.tensor_scalar(
-                out=yv_all[:, s, :, :], in0=yv_all[:, s, :, :], scalar1=4.0, scalar2=None,
-                op0=ALU.min,
+                out=yv_all[:, first:last, :, :], in0=yv_all[:, first:last, :, :], scalar1=4.0,
+                scalar2=None, op0=ALU.min,
             )
 
         def to_rows(bank, source, lo):
@@ -454,53 +459,59 @@ def tile_chainlveg_pa_t_kernel(
             nc.sync.dma_start(out=scale_rows[:, tiles_of(s), :], in_=scale[:])
 
         nc.scalar.activation(
-            out=as_njtg(half_inv_a), in_=repeat_t(svar), func=ACT.Exp, scale=-2.0
+            out=as_njtg(half_inv_a), in_=repeat_t(svar), func=ACT.Exp, scale=-2.0,
+            bias=-math.log(2.0),
         )
         offset_selector()
         spread_var()
-        widen_var(0)
+        widen_var(0, 2)
         transpose_x(0)
         nc.scalar.activation(out=spare[:], in_=two[:], func=ACT.Sigmoid)
         bias_to_partitions()
         group_weights(1)
-        quantise_x(0)
+        bias_offsets()
         quantise_weights(1)
+        quantise_x(0)
         pack_state()
-        widen_var(1)
         group_weights(0)
         quantise_weights(0)
         for s in range(UNITS):
-            u = (s - 1) // 2
+            u = s // 2
+            odd = s % 2 == 1
             if 4 <= s + 3 < UNITS:
                 load_x(s + 3, 1)
             project(s, 1)
-            if s % 2 == 1:
+            if odd:
                 turn_wc(u)
             turn_v1(s)
             if s == 0:
                 transpose_x(1)
                 spread_mu()
             project(s, 0)
-            if s + 2 < UNITS:
+            if 0 < s and s + 2 < UNITS:
                 transpose_x(s + 2)
-            if s == 1:
+            if s == UNITS - 2:
                 turn_state()
-            if s % 2 == 1:
+            if odd:
                 sub_dn(u)
                 sub_product(u)
             elif s > 0:
-                sub_mean(u)
-                sub_square(u)
+                sub_mean(u - 1)
+                sub_square(u - 1)
             difference(s)
             sigmoid(s)
-            if s % 2 == 0:
-                turn_m(s // 2)
-            if s + 1 < UNITS:
+            if s == 0:
+                transpose_x(2)
+                quantise_x(1)
+                clip_v(0, 1)
+            if not odd:
+                turn_m(u)
+            elif s + 1 < UNITS:
                 quantise_x(s + 1)
-            if s < ADDED_FROM:
-                clip_v(s)
-            if s + 2 < UNITS:
-                widen_var(s + 2)
+                clip_v(max(s - 1, 1), s + 1)
+                widen_var(s + 1, 2)
+                quantise_x(s + 2)
+        clip_v(UNITS - 2, UNITS - 1)
         turn_m(EARLY)
         for w in range(EARLY):
             log_weight(w)

@@ -525,13 +525,12 @@ def tile_chainlveg_pa_t_kernel(
         for u in range(EARLY, UNITS):
             if u + 1 < UNITS:
                 turn_m(u + 1)
-                turn_wc(u + 1)
                 sub_dn(u + 1)
+            variance(ready)
+            if u + 1 < UNITS:
+                turn_wc(u + 1)
                 sub_product(u + 1)
                 log_weight(u + 1)
-            if ready >= ADDED_FROM:
-                clip_and_add(ready)
-            variance(ready)
             sum_logs(ready)
             sub_mean(u)
             if ready + 1 >= ADDED_FROM:

import math
from contextlib import ExitStack

import concourse.masks as masks
import concourse.mybir as mybir

F32 = mybir.dt.float32
BF16 = mybir.dt.bfloat16
U32 = mybir.dt.uint32
U8 = mybir.dt.uint8
FP8X4 = mybir.dt.float8_e4m3fn_x4
ALU = mybir.AluOpType
ACT = mybir.ActivationFunctionType

FLOPS = 2 * 4096 * 512 * 512

P = 128
TILES = 32
UNIT = 4
UNITS = TILES // UNIT
ROWS = UNIT * P
K = 512
NC = 256
NI = 8
JTG = NC // NI
JT = JTG // 2
HALF = UNIT // 2
BANKS_SCALAR = 4
EARLY = 4
VAR_BIAS = 0.5 * math.log(2.0 * math.pi) - 1.0
ADDED_FROM = 7
SLOTS = 32


def tile_chainlveg_pa_t_kernel(
    tc, x, s_weight, s_mu, s_var, tcm_w, tcm_b, tcv_w, tcv_b, out_0, out_1, out_2
):
    nc = tc.nc
    x_rows = x.rearrange("b (c n) k -> (b c) n k", n=TILES)
    scale_rows = out_0.rearrange("b (c n) i j t e -> (b c) n (i j t e)", n=TILES)
    mu_rows = out_1.rearrange("b (c n) i j t e g -> (b c) n (i j t e g)", n=TILES)
    var_rows = out_2.rearrange("b (c n) i j t e g -> (b c) n (i j t e g)", n=TILES)

    with ExitStack() as ctx:
        keep = ctx.enter_context(tc.tile_pool(name="keep", bufs=1))
        x_pool = ctx.enter_context(tc.tile_pool(name="xs", bufs=4))
        grouped_pool = ctx.enter_context(tc.tile_pool(name="grouped", bufs=2))
        xq_pool = ctx.enter_context(tc.tile_pool(name="xq", bufs=4))
        wide_pool = ctx.enter_context(tc.tile_pool(name="wide", bufs=2))
        am_pool = ctx.enter_context(tc.tile_pool(name="am", bufs=6))
        row_pool = ctx.enter_context(tc.tile_pool(name="rows", bufs=3))
        da_pool = ctx.enter_context(tc.tile_pool(name="da", bufs=2))
        out_pool = ctx.enter_context(tc.tile_pool(name="outs", bufs=3))
        psum_s = ctx.enter_context(tc.psum_pool(name="psum_s", bufs=BANKS_SCALAR))
        psum_v = ctx.enter_context(tc.psum_pool(name="psum_v", bufs=8 - BANKS_SCALAR))
        ctx.enter_context(tc.manual_schedule())

        def tiles_of(s):
            return slice(s * UNIT, (s + 1) * UNIT)

        alive = {}

        w_raw = keep.tile([P, 4, 2 * NC], BF16, name="w_raw")
        bias_rows = keep.tile([P, NC], BF16, name="bias_rows")
        smu = keep.tile([P, TILES * 16], BF16, name="smu")
        svar = keep.tile([P, TILES * 16], BF16, name="svar")
        sw = keep.tile([P, TILES * 8], BF16, name="sw")
        two = keep.tile([P, 1], F32, name="two")
        nc.vector.memset(two[:], 2.0)
        spare = keep.tile([P, 1], F32, name="spare")
        nc.scalar.activation(out=spare[:], in_=two[:], func=ACT.Exp)
        nc.vector.memset(bias_rows[:], 0.0)

        def load_x(s, pieces):
            tile = x_pool.tile([P, UNIT, K], BF16, name="x_sb")
            alive[("x", s)] = tile
            step = UNIT // pieces
            for lo in range(0, UNIT, step):
                n = s * UNIT + lo
                nc.sync.dma_start(out=tile[:, lo : lo + step, :], in_=x_rows[:, n : n + step, :])

        def load_w(w, first_column):
            nc.sync.dma_start(
                out=w_raw[:, :, first_column : first_column + NC],
                in_=w.rearrange("(q t) c -> q t c", t=4),
            )

        nc.scalar.dma_start(
            out=svar[:], in_=s_var.rearrange("b (c n) j e g -> (b c) (n j e g)", n=TILES)
        )
        nc.scalar.dma_start(out=bias_rows[0:1, :], in_=tcm_b.rearrange("(r c) -> r c", r=1))
        nc.scalar.dma_start(out=bias_rows[1:2, :], in_=tcv_b.rearrange("(r c) -> r c", r=1))
        load_x(0, 2)
        load_w(tcv_w, NC)
        nc.scalar.dma_start(
            out=smu[:], in_=s_mu.rearrange("b (c n) j e g -> (b c) (n j e g)", n=TILES)
        )
        load_w(tcm_w, 0)
        nc.sync.dma_start(
            out=sw[:], in_=s_weight.rearrange("b (c n) j e -> (b c) (n j e)", n=TILES)
        )
        load_x(1, 1)
        load_x(2, 1)
        load_x(3, 1)

        ident = keep.tile([P, P], F32, name="ident")
        masks.make_identity(nc, ident[:])
        ident_bf16 = keep.tile([P, P], BF16, name="ident_bf16")
        nc.gpsimd.tensor_copy(out=ident_bf16[:], in_=ident[:])
        packed = keep.tile([P, TILES, SLOTS], BF16, name="packed")
        nc.vector.memset(packed[:], 0.0)
        w_grouped = keep.tile([P, 2, 2, P, 4], BF16, name="w_grouped", align_bytes=64)
        w_codes = keep.tile([P, 2 * NC], U32, name="w_codes", align_bytes=64)
        w_scales = keep.tile([P, 2 * NC], U8, name="w_scales", align_bytes=64)
        bias_f32 = keep.tile([P, 2, P], F32, name="bias_f32")
        bias_m = keep.tile([P, 2], F32, name="bias_m")
        bias_v = keep.tile([P, 2], F32, name="bias_v")
        yv_all = keep.tile([P, UNITS, 2, ROWS], F32, name="yv_all")
        wc_all = keep.tile([P, UNITS, 2, ROWS], F32, name="wc_all")
        m1 = keep.tile([P, TILES, JTG], BF16, name="m1")
        m1_plus_1 = keep.tile([P, TILES, JTG], F32, name="m1_plus_1")
        half_inv_a = keep.tile([P, TILES, JTG], F32, name="half_inv_a")
        two_v1 = keep.tile([P, TILES, JTG], BF16, name="two_v1")
        packed_t = keep.tile([P, UNITS, P], BF16, name="packed_t")
        picks = keep.tile([P, UNIT, 8], BF16, name="picks")
        picks_v = keep.tile([P, UNIT, 8], BF16, name="picks_v")
        select_offset = keep.tile([P, UNIT, P], BF16, name="select_offset")
        sums = keep.tile([P, TILES, P], F32, name="sums")

        def halves(s):
            return [(lo, s * UNIT + lo) for lo in range(0, UNIT, HALF)]

        def repeat_t(small):
            return (
                small[:]
                .rearrange("p (a g) -> p a g", g=2)
                .unsqueeze(2)
                .to_broadcast([P, TILES * 8, 2, 2])
            )

        def as_njtg(full):
            return full[:].rearrange("p n (j t g) -> p (n j) t g", t=2, g=2)

        def repeat_i(small, n, count):
            return small[:, n : n + count, :].unsqueeze(2).to_broadcast([P, count, NI, JTG])

        def by_tile_and_i(ap, count):
            return ap.rearrange("p (n i c) -> p n i c", n=count, i=NI)

        def group_weights(which):
            raw = w_raw[:, :, which * NC : (which + 1) * NC].rearrange(
                "p t (c g) -> p g c t", g=2
            )
            for g in range(2):
                nc.vector.tensor_copy(out=w_grouped[:, which, g, :, :], in_=raw[:, g])

        def quantise_weights(which):
            columns = slice(which * NC, (which + 1) * NC)
            nc.vector.quantize_mx(
                out=w_codes[:, columns].bitcast(FP8X4),
                scales=w_scales[:, columns],
                in_=w_grouped[:, which, :, :, :].rearrange("p g c t -> p (g c t)"),
            )

        def bias_to_partitions():
            nc.vector.tensor_copy(
                out=bias_f32[:], in_=bias_rows[:].rearrange("p (c g) -> p g c", g=2)
            )
            turned = psum_s.tile([P, 512], F32, name="turned", tag="to_scalar")
            for g in range(2):
                nc.tensor.transpose(turned[:, g * P : (g + 1) * P], bias_f32[:, g, :], ident[:])
            alive["bias_rows"] = turned

        def bias_offsets():
            turned = alive["bias_rows"]
            by_row = turned[:, 0 : 2 * P].rearrange("p (g r) -> p r g", g=2)
            nc.vector.tensor_scalar_add(out=bias_m[:], in0=by_row[:, 0, :], scalar1=1.0)
            nc.vector.tensor_scalar(
                out=bias_v[:], in0=by_row[:, 1, :], scalar1=2.0, scalar2=2.0,
                op0=ALU.mult, op1=ALU.add,
            )

        def widen_var(first, units):
            wide_v1 = wide_pool.tile([P, units * UNIT, NC], BF16, name="wide_v1")
            for s in range(units):
                alive[("wide", first + s)] = wide_v1[:, tiles_of(s), :]
            rows = slice(first * UNIT, (first + units) * UNIT)
            nc.vector.tensor_copy(
                out=wide_v1[:].rearrange("p n (i c) -> p n i c", i=NI),
                in_=two_v1[:, rows, :].unsqueeze(2).to_broadcast([P, units * UNIT, NI, JTG]),
            )

        def spread_var():
            nc.vector.tensor_scalar(
                out=as_njtg(two_v1), in0=repeat_t(svar), scalar1=2.0, scalar2=None, op0=ALU.mult
            )

        def spread_mu():
            nc.vector.tensor_copy(out=as_njtg(m1), in_=repeat_t(smu))
            nc.vector.tensor_scalar_add(out=m1_plus_1[:], in0=m1[:], scalar1=1.0)

        def offset_selector():
            by_slot = ident_bf16[:].rearrange("p (n c) -> p n c", c=SLOTS)
            nc.gpsimd.tensor_tensor(
                out=picks_v[:], in0=by_slot[:, :, 8:24:2], in1=by_slot[:, :, 9:24:2], op=ALU.add
            )
            nc.gpsimd.tensor_tensor(
                out=picks[:], in0=by_slot[:, :, 0:8], in1=picks_v[:], op=ALU.subtract
            )
            for lo in range(UNIT):
                nc.gpsimd.tensor_scalar(
                    out=select_offset[:, lo, :].rearrange("p (i j t) -> p i j t", i=NI, t=2),
                    in0=picks[:, lo, :].unsqueeze(1).unsqueeze(3).to_broadcast([P, NI, 8, 2]),
                    scalar1=2.0, scalar2=0.0, op0=ALU.mult, op1=ALU.add,
                )

        def pack_state():
            nc.scalar.copy(
                out=packed[:, :, 0:8], in_=sw[:].rearrange("p (n j) -> p n j", j=8)
            )
            nc.scalar.copy(
                out=packed[:, :, 8:24], in_=svar[:].rearrange("p (n c) -> p n c", c=16)
            )

        def turn_state():
            turned = psum_s.tile([P, UNITS, P], BF16, name="packed_turned", tag="to_scalar")
            for s in range(UNITS):
                nc.tensor.transpose(
                    turned[:, s, :],
                    packed[:, tiles_of(s), :].rearrange("p n c -> p (n c)"),
                    ident_bf16[:],
                )
            nc.scalar.copy(out=packed_t[:], in_=turned[:])

        def transpose_x(s):
            grouped = grouped_pool.tile([P, 4 * ROWS], BF16, name="grouped", align_bytes=64)
            alive[("grouped", s)] = grouped
            for lo in range(0, UNIT, 2):
                turned = psum_s.tile([P, 2, 2 * P], F32, name="x_turned", tag="to_scalar")
                for j in range(2):
                    words = alive[("x", s)][:, lo + j, :].bitcast(F32)
                    for u in range(2):
                        nc.tensor.transpose(
                            turned[:, u, j * P : (j + 1) * P],
                            words[:, u : 2 * P : 2],
                            ident[:],
                        )
                nc.scalar.copy(
                    out=grouped[:].bitcast(F32)[:, lo * 2 * P : (lo + 2) * 2 * P].rearrange(
                        "p (r u) -> p r u", u=2
                    ),
                    in_=turned[:].rearrange("p u r -> p r u"),
                )

        def quantise_x(s):
            codes = xq_pool.tile([P, ROWS], U32, name="x_codes", align_bytes=64)
            scales = xq_pool.tile([P, ROWS], U8, name="x_scales", align_bytes=64)
            alive[("xq", s)] = (codes, scales)
            nc.vector.quantize_mx(
                out=codes[:].bitcast(FP8X4), scales=scales[:], in_=alive[("grouped", s)][:]
            )

        def project(s, which):
            codes, scales = alive[("xq", s)]
            if which == 0:
                alive[("am", s)] = am_pool.tile([P, 2, ROWS], F32, name="am")
            for g in range(2):
                if True:
                    first = which * NC + g * P
                    product = psum_s.tile([P, ROWS], F32, name="product", tag="to_scalar")
                    nc.tensor.matmul_mx(
                        out=product[:],
                        lhsT=w_codes[:, first : first + P].bitcast(FP8X4),
                        lhsT_scale=w_scales[:, first : first + P],
                        rhs=codes[:].bitcast(FP8X4),
                        rhs_scale=scales[:],
                        start=True,
                        stop=True,
                    )
                    if which == 1:
                        nc.scalar.activation(
                            out=yv_all[:, s, g, :], in_=product[:], func=ACT.Relu,
                            bias=bias_v[:, g : g + 1], scale=2.0,
                        )
                    else:
                        nc.scalar.activation(
                            out=alive[("am", s)][:, g, :], in_=product[:], func=ACT.Relu,
                            bias=bias_m[:, g : g + 1], scale=1.0,
                        )

        def turn_v1(s):
            turned = psum_v.tile([P, ROWS], F32, name="v1_turned", tag="to_vector")
            alive[("v1", s)] = turned
            for lo in range(UNIT):
                nc.tensor.transpose(
                    turned[:, lo * P : (lo + 1) * P],
                    alive[("wide", s)][:, lo, :].bitcast(F32),
                    ident[:],
                )

        def difference(s):
            nc.vector.scalar_tensor_tensor(
                out=wc_all[:, s, :, :], in0=yv_all[:, s, :, :], scalar=4.0, in1=alive[("v1", s)][:].bitcast(BF16).rearrange("p (r g) -> p g r", g=2),
                op0=ALU.min, op1=ALU.subtract,
            )

        def sigmoid(s):
            nc.scalar.activation(
                out=wc_all[:, s, :, :], in_=wc_all[:, s, :, :], func=ACT.Sigmoid, bias=two[:],
                scale=-1.0,
            )

        def clip_and_add(s):
            nc.vector.scalar_tensor_tensor(
                out=yv_all[:, s, :, :], in0=yv_all[:, s, :, :], scalar=4.0,
                in1=wc_all[:, s, :, :], op0=ALU.min, op1=ALU.add,
            )

        def clip_v(first, last):
            nc.vector.tensor_scalar(
                out=yv_all[:, first:last, :, :], in0=yv_all[:, first:last, :, :], scalar1=4.0,
                scalar2=None, op0=ALU.min,
            )

        def to_rows(bank, source, lo):
            for j in range(HALF):
                for g in range(2):
                    nc.tensor.transpose(
                        bank[:, j, g, :], source[:, g, (lo + j) * P : (lo + j + 1) * P], ident[:]
                    )

        def turn_m(s):
            for lo in range(0, UNIT, HALF):
                bank = psum_v.tile([P, HALF, 2, P], F32, name="m_rows", tag="to_vector")
                to_rows(bank, alive[("am", s)], lo)
                alive[("m_rows", s, lo)] = bank

        def sub_dn(s):
            dn = row_pool.tile([P, UNIT * NC], F32, name="dn")
            da = da_pool.tile([P, UNIT * NC], F32, name="da")
            alive[("dn", s)] = dn
            alive[("da", s)] = da
            for lo, n in halves(s):
                bank = alive[("m_rows", s, lo)]
                part = slice(lo * NC, (lo + HALF) * NC)
                for j in range(HALF):
                    nc.vector.scalar_tensor_tensor(
                        out=dn[:, (lo + j) * NC : (lo + j + 1) * NC].rearrange(
                            "p (i c g) -> p i c g", i=NI, g=2
                        ),
                        in0=bank[:, j, :, :].rearrange("p g (i c) -> p i c g", i=NI),
                        scalar=2.0,
                        in1=m1_plus_1[:, n + j, :]
                        .rearrange("p (c g) -> p c g", g=2)
                        .unsqueeze(1)
                        .to_broadcast([P, NI, JT, 2]),
                        op0=ALU.min,
                        op1=ALU.subtract,
                    )
                nc.gpsimd.tensor_tensor(
                    out=by_tile_and_i(da[:, part], HALF), in0=by_tile_and_i(dn[:, part], HALF),
                    in1=repeat_i(half_inv_a, n, HALF), op=ALU.mult,
                )

        def turn_wc(s):
            for lo in range(0, UNIT, HALF):
                bank = psum_v.tile([P, HALF, 2, P], F32, name="wc_rows", tag="to_vector")
                to_rows(bank, wc_all[:, s, :, :], lo)
                alive[("wc_rows", s, lo)] = bank

        def sub_product(s):
            g_tile = row_pool.tile([P, UNIT * NC], F32, name="g_tile")
            alive[("g", s)] = g_tile
            for lo, n in halves(s):
                bank = alive[("wc_rows", s, lo)]
                part = slice(lo * NC, (lo + HALF) * NC)
                nc.vector.tensor_tensor(
                    out=g_tile[:, part].rearrange("p (n c g) -> p n c g", n=HALF, g=2),
                    in0=bank[:].rearrange("p n g c -> p n c g"),
                    in1=alive[("dn", s)][:, part].rearrange("p (n c g) -> p n c g", n=HALF, g=2),
                    op=ALU.mult,
                )

        def sub_square(s):
            dn = alive[("dn", s)]
            nc.vector.tensor_tensor(
                out=dn[:], in0=alive[("g", s)][:], in1=alive[("da", s)][:], op=ALU.mult
            )
            pair = dn[:].rearrange("p (n c g) -> p n c g", n=UNIT, g=2)
            nc.gpsimd.tensor_tensor(
                out=sums[:, tiles_of(s), :], in0=pair[:, :, :, 0], in1=pair[:, :, :, 1], op=ALU.add
            )

        def sub_mean(s):
            mu = out_pool.tile([P, UNIT * NC], F32, name="mu", bufs=2)
            nc.vector.tensor_tensor(
                out=by_tile_and_i(mu[:], UNIT), in0=by_tile_and_i(alive[("g", s)][:], UNIT),
                in1=repeat_i(m1, s * UNIT, UNIT), op=ALU.add,
            )
            nc.sync.dma_start(
                out=mu_rows[:, tiles_of(s), :], in_=mu[:].rearrange("p (n c) -> p n c", n=UNIT)
            )

        def log_weight(s):
            nc.scalar.activation(
                out=wc_all[:, s, :, :], in_=wc_all[:, s, :, :], func=ACT.Ln,
                scale=0.5 / math.pi,
            )

        def variance(s, on_vector=False):
            var = out_pool.tile([P, UNIT, NC], F32, name="var")
            for lo, n in halves(s):
                bank = psum_s.tile([P, HALF, 2, P], F32, name="var_rows", tag="to_scalar")
                for j in range(HALF):
                    rows = slice((lo + j) * P, (lo + j + 1) * P)
                    for g in range(2):
                        if s >= ADDED_FROM:
                            nc.tensor.transpose(
                                bank[:, j, g, :], yv_all[:, s, g, rows], ident[:]
                            )
                            continue
                        nc.tensor.matmul(
                            bank[:, j, g, :], lhsT=wc_all[:, s, g, rows], rhs=ident[:],
                            is_transpose=True, start=True, stop=False,
                        )
                        nc.tensor.matmul(
                            bank[:, j, g, :], lhsT=yv_all[:, s, g, rows], rhs=ident[:],
                            is_transpose=True, start=False, stop=True,
                        )
                nc.scalar.activation(
                    out=var[:, lo : lo + HALF, :].rearrange("p n (c g) -> p n c g", g=2),
                    in_=bank[:].rearrange("p n g c -> p n c g"),
                    func=ACT.Copy, bias=VAR_BIAS, scale=0.5,
                )
            nc.sync.dma_start(out=var_rows[:, tiles_of(s), :], in_=var[:])

        def sum_logs(s):
            bank = psum_v.tile([P, UNIT, P], F32, name="sum_rows", tag="to_vector")
            alive[("sum_rows", s)] = bank
            for lo in range(UNIT):
                rows = slice(lo * P, (lo + 1) * P)
                nc.tensor.matmul(
                    bank[:, lo, :], lhsT=packed_t[:, s, :], rhs=select_offset[:, lo, :],
                    start=True, stop=False,
                )
                for g in range(2):
                    nc.tensor.matmul(
                        bank[:, lo, :], lhsT=wc_all[:, s, g, rows], rhs=ident[:],
                        is_transpose=True, start=False, stop=(g == 1),
                    )

        def log_scale(s):
            scale = out_pool.tile([P, UNIT, P], F32, name="scale")
            bank = alive[("sum_rows", s)]
            nc.vector.scalar_tensor_tensor(
                out=scale[:], in0=bank[:], scalar=0.5, in1=sums[:, tiles_of(s), :],
                op0=ALU.mult, op1=ALU.subtract,
            )
            nc.sync.dma_start(out=scale_rows[:, tiles_of(s), :], in_=scale[:])

        nc.scalar.activation(
            out=as_njtg(half_inv_a), in_=repeat_t(svar), func=ACT.Exp, scale=-2.0,
            bias=-math.log(2.0),
        )
        offset_selector()
        spread_var()
        widen_var(0, 2)
        transpose_x(0)
        nc.scalar.activation(out=spare[:], in_=two[:], func=ACT.Sigmoid)
        bias_to_partitions()
        group_weights(1)
        bias_offsets()
        quantise_weights(1)
        quantise_x(0)
        pack_state()
        group_weights(0)
        quantise_weights(0)
        for s in range(UNITS):
            u = s // 2
            odd = s % 2 == 1
            if 4 <= s + 3 < UNITS:
                load_x(s + 3, 1)
            project(s, 1)
            if odd:
                turn_wc(u)
            turn_v1(s)
            if s == 0:
                transpose_x(1)
                spread_mu()
            project(s, 0)
            if 0 < s and s + 2 < UNITS:
                transpose_x(s + 2)
            if s == UNITS - 2:
                turn_state()
            if odd:
                sub_dn(u)
                sub_product(u)
            elif s > 0:
                sub_mean(u - 1)
                sub_square(u - 1)
            difference(s)
            sigmoid(s)
            if s == 0:
                transpose_x(2)
                quantise_x(1)
                clip_v(0, 1)
            if not odd:
                turn_m(u)
            elif s + 1 < UNITS:
                quantise_x(s + 1)
                clip_v(max(s - 1, 1), s + 1)
                widen_var(s + 1, 2)
                quantise_x(s + 2)
        clip_v(UNITS - 2, UNITS - 1)
        turn_m(EARLY)
        for w in range(EARLY):
            log_weight(w)
        sub_dn(EARLY)
        turn_wc(EARLY)
        sub_product(EARLY)
        log_weight(EARLY)
        sub_mean(EARLY - 1)
        sub_square(EARLY - 1)
        ready = 0
        for u in range(EARLY, UNITS):
            if u + 1 < UNITS:
                turn_m(u + 1)
                sub_dn(u + 1)
            variance(ready)
            if u + 1 < UNITS:
                turn_wc(u + 1)
                sub_product(u + 1)
                log_weight(u + 1)
            sum_logs(ready)
            sub_mean(u)
            if ready + 1 >= ADDED_FROM:
                clip_and_add(ready + 1)
            sub_square(u)
            log_scale(ready)
            variance(ready + 1)
            sum_logs(ready + 1)
            log_scale(ready + 1)
            ready += 2
